import numpy as np
import ml_dtypes


def mxq(x, axis, fmt="e4m3"):
    dtype, down = {"e4m3": (ml_dtypes.float8_e4m3fn, 7), "e5m2": (ml_dtypes.float8_e5m2, 14)}[fmt]
    v = np.moveaxis(np.asarray(x, np.float32).astype(ml_dtypes.bfloat16).astype(np.float64), axis, -1)
    blocks = v.reshape(v.shape[:-1] + (-1, 32))
    amax = np.abs(blocks).max(-1, keepdims=True)
    byte = np.maximum(np.where(amax > 0, np.frexp(amax)[1] - 1 + 127, 0) - down, 1)
    scale = np.exp2(byte - 127.0)
    codes = (blocks / scale).astype(np.float32).astype(dtype).astype(np.float64)
    return np.moveaxis((codes * scale).reshape(v.shape), -1, axis)


WIDE = False


def mx_kscale(k):
    if not WIDE:
        return np.ones(k)
    levels = np.array([10, -10, 5, -5, 0])
    if k % 512:
        return np.exp2(np.random.permutation(np.resize(levels, k // 32))).repeat(32)
    a = np.empty((k // 512, 16))
    for p in range(k // 512):
        a[p, :8] = np.random.permutation(np.resize(levels, 8))
        for g in range(8):
            far = levels[np.abs(levels - a[p, g]) >= 10]
            a[p, g + 8] = far[np.random.randint(len(far))]
    return np.exp2(a.ravel()).repeat(32)


BF16 = ml_dtypes.bfloat16


def bf(x):
    return np.asarray(x, np.float32).astype(BF16)


def f64(x):
    return np.asarray(x).astype(np.float64)


B, S, H, D = 2, 2048, 8, 64
E = H * D
HALF = D // 2


def rotate_half(u):
    u1, u2 = np.split(u, 2, axis=-1)
    return np.concatenate([-u2, u1], axis=-1)


def apply_rope(t, sin, cos):
    x1, x2 = np.split(t, 2, axis=-1)
    x_rot = x1 * cos + rotate_half(x1) * sin
    return np.concatenate([x_rot, x2], axis=-1)


def setup_inputs():
    s = mx_kscale(E)
    th = np.random.uniform(0.0, 2.0 * np.pi, (S, HALF))
    return {"x": bf(np.random.standard_normal((B, S, E)) * s),
            "W_qkv": bf(np.random.standard_normal((E, 3 * E)) / np.sqrt(E) / s[:, None]),
            "b_qkv": bf(np.random.standard_normal(3 * E) * 0.2),
            "sin_tab": bf(np.sin(th)),
            "cos_tab": bf(np.cos(th))}


def reference(x, W_qkv, b_qkv, sin_tab, cos_tab):
    qkv = (mxq(f64(x), 2, "e4m3") @ mxq(f64(W_qkv), 0, "e4m3")) + f64(b_qkv)
    q, k, v = np.split(qkv, 3, axis=-1)
    q = q.reshape(B, S, H, D)
    k = k.reshape(B, S, H, D)
    v = v.reshape(B, S, H, D)
    sin = f64(sin_tab)[None, :, None, :]
    cos = f64(cos_tab)[None, :, None, :]
    q_rot = apply_rope(q, sin, cos)
    k_rot = apply_rope(k, sin, cos)
    return q_rot, k_rot, v

@@ -1,0 +1,354 @@
+from contextlib import ExitStack
+
+import concourse.mybir as mybir
+from concourse.masks import make_identity
+
+F32 = mybir.dt.float32
+BF16 = mybir.dt.bfloat16
+U32 = mybir.dt.uint32
+U8 = mybir.dt.uint8
+FP8X4 = mybir.dt.float8_e4m3fn_x4
+ALU = mybir.AluOpType
+
+P = 128
+TOKENS = 4096
+E = 512
+GROUPS = 8
+T = 4
+FLOPS = 2 * TOKENS * E * 3 * E
+
+ROT, PAS, VAL = 0, 512, 1024
+
+
+def tile_improvedattention_pa_t_kernel(
+    tc, x, W_qkv, b_qkv, sin_tab, cos_tab, out_0, out_1, out_2
+):
+    nc = tc.nc
+    xf = x.flatten_outer_dims()
+    outs = [o.rearrange("b s h d -> (b s) (h d)") for o in (out_0, out_1, out_2)]
+
+    with ExitStack() as ctx:
+        const = ctx.enter_context(tc.tile_pool(name="const", bufs=1))
+        xin = ctx.enter_context(tc.tile_pool(name="xin", bufs=GROUPS))
+        xgr = ctx.enter_context(tc.tile_pool(name="xgr", bufs=2))
+        xq = ctx.enter_context(tc.tile_pool(name="xq", bufs=3))
+        mwp = ctx.enter_context(tc.tile_pool(name="mwp", bufs=2))
+        oqkp = ctx.enter_context(tc.tile_pool(name="oqkp", bufs=3))
+        ovp = ctx.enter_context(tc.tile_pool(name="ovp", bufs=3))
+        psr = ctx.enter_context(tc.psum_pool(name="psr", bufs=2))
+        psa = ctx.enter_context(tc.psum_pool(name="psa", bufs=3))
+        pst = ctx.enter_context(tc.psum_pool(name="pst", bufs=3))
+        ctx.enter_context(nc.allow_non_contiguous_dma(reason="short rows of tables and column chunks"))
+        ctx.enter_context(tc.manual_schedule())
+
+        bnat = const.tile([P, 3 * E], BF16, name="bnat")
+        nc.vector.memset(bnat[:], 0.0)
+        ctab = const.tile([P, 16, 32], BF16, name="ctab")
+        stab = const.tile([P, 16, 32], BF16, name="stab")
+        nc.scalar.dma_start(out=bnat[0:1, :], in_=b_qkv.rearrange("(o c) -> o c", o=1))
+        for tab_sb, tab in ((stab, sin_tab), (ctab, cos_tab)):
+            nc.scalar.dma_start(
+                out=tab_sb[:].rearrange("p (g t) j -> p g (t j)", g=4),
+                in_=tab.rearrange("(g p t) j -> p g (t j)", g=4, p=P, t=T),
+            )
+
+        x_sb = []
+        for g in range(GROUPS):
+            x_sb.append(xin.tile([P, T * E], BF16, name="x_sb%d" % g, tag="x_sb"))
+
+        def load_x(g):
+            nc.sync.dma_start(
+                out=x_sb[g][:],
+                in_=xf[512 * g : 512 * (g + 1), :].rearrange("(p t) k -> p (t k)", t=T),
+            )
+
+        wraw = const.tile([P, 4, 3 * E], BF16, name="wraw")
+
+        def load_w(c0):
+            nc.sync.dma_start(
+                out=wraw[:, :, c0 : c0 + 512],
+                in_=W_qkv[:, c0 : c0 + 512].rearrange("(q t) c -> q t c", t=4),
+            )
+
+        load_x(0)
+        load_w(1024)
+        load_w(0)
+        load_w(512)
+        for g in range(1, GROUPS):
+            load_x(g)
+
+        ident_f = const.tile([P, P], F32, name="ident_f")
+        make_identity(nc, ident_f[:])
+        ident_b = const.tile([P, P], BF16, name="ident_b")
+        make_identity(nc, ident_b[:])
+        ones_b = const.tile([P, P], BF16, name="ones_b")
+        nc.vector.memset(ones_b[:], 1.0)
+        perm_f = const.tile([P, P], F32, name="perm_f")
+        id4 = ident_f[:].rearrange("p (a w i) -> p a w i", a=4, w=2)
+        pm4 = perm_f[:].rearrange("p (a w i) -> p a w i", a=4, w=2)
+        nc.vector.tensor_copy(out=pm4[:, :, 0, :], in_=id4[:, :, 1, :])
+        nc.vector.tensor_copy(out=pm4[:, :, 1, :], in_=id4[:, :, 0, :])
+
+        xc = {}
+        xs = {}
+        xbanks = {}
+        xgrouped = {}
+
+        def x_transposes(g):
+            xw = x_sb[g][:].bitcast(F32)
+            banks = []
+            for hf in range(2):
+                xt = pst.tile([P, 4, P], F32, name="xt", tag="t")
+                for tt in range(2):
+                    for u in range(2):
+                        c0 = 256 * (2 * hf + tt)
+                        nc.tensor.transpose(xt[:, 2 * tt + u, :], xw[:, c0 + u : c0 + 256 : 2], ident_f[:])
+                banks.append(xt)
+            xbanks[g] = banks
+
+        def x_copy_out(g):
+            grouped = xgr.tile([P, 4 * 512], BF16, name="grouped", tag="grouped", align_bytes=64)
+            g32 = grouped[:].bitcast(F32)
+            for hf in range(2):
+                nc.scalar.copy(
+                    out=g32[:, 512 * hf : 512 * (hf + 1)].rearrange(
+                        "q (tt p u) -> q tt p u", tt=2, p=P, u=2
+                    ),
+                    in_=xbanks[g][hf][:].rearrange("q (tt u) p -> q tt p u", tt=2, u=2),
+                )
+            xgrouped[g] = grouped
+
+        def x_quantise(g):
+            codes = xq.tile([P, 512], U32, name="xcodes", tag="xcodes", align_bytes=64)
+            scales = xq.tile([P, 512], U8, name="xscales", tag="xscales", align_bytes=64)
+            nc.vector.quantize_mx(out=codes[:].bitcast(FP8X4), scales=scales[:], in_=xgrouped[g][:])
+            xc[g] = codes
+            xs[g] = scales
+
+        brow = const.tile([P, 1024], BF16, name="brow")
+        bqk = bnat[:, 0:1024].rearrange("p (g w j) -> p w g j", g=16, w=2)
+        nc.vector.tensor_copy(out=brow[:, 512:1024].rearrange("p (g j) -> p g j", g=16), in_=bqk[:, 1])
+        nc.vector.tensor_copy(out=brow[:, 0:512].rearrange("p (g j) -> p g j", g=16), in_=bqk[:, 0])
+        pbs = []
+        for rhs in (brow[:, 512:1024], bnat[:, 1024:1536]):
+            pb = psa.tile([P, 512], F32, name="pb", tag="a")
+            nc.tensor.matmul(pb[:], lhsT=ones_b[:], rhs=rhs, start=True, stop=True)
+            pbs.append(pb)
+        pbt = psa.tile([P, 512], F32, name="pbt", tag="a")
+        for i in range(4):
+            nc.tensor.matmul(
+                pbt[:, 32 * i : 32 * (i + 1)], lhsT=brow[:, P * i : P * (i + 1)], rhs=ones_b[:, 0:32],
+                start=True, stop=True,
+            )
+
+        csrep = const.tile([P, 2, 16, P], BF16, name="csrep")
+        csT = const.tile([P, 2, 2048], BF16, name="csT")
+        crep = csrep[:, 0].rearrange("p a (r j) -> p a r j", r=4)
+        srep = csrep[:, 1].rearrange("p a (r w i) -> p a r w i", r=4, w=2)
+
+        def spread(tab_part, n, width):
+            return tab_part.unsqueeze(2).to_broadcast([P, n, 4, width])
+
+        nc.vector.tensor_copy(out=srep[:, 0:4, :, 0, :], in_=spread(stab[:, 0:4, 16:32], 4, 16))
+        nc.vector.tensor_scalar_mul(
+            out=srep[:, 0:4, :, 1, :], in0=spread(stab[:, 0:4, 0:16], 4, 16), scalar1=-1.0
+        )
+        nc.scalar.copy(out=crep[:, 0:4], in_=spread(ctab[:, 0:4, :], 4, 32))
+        nc.gpsimd.tensor_scalar(
+            out=crep[:, 4:16], in0=spread(ctab[:, 4:16, :], 12, 32),
+            scalar1=1.0, scalar2=0.0, op0=ALU.mult, op1=ALU.add,
+        )
+        nc.gpsimd.tensor_scalar(
+            out=srep[:, 4:16, :, 0, :], in0=spread(stab[:, 4:16, 16:32], 12, 16),
+            scalar1=1.0, scalar2=0.0, op0=ALU.mult, op1=ALU.add,
+        )
+        nc.gpsimd.tensor_scalar(
+            out=srep[:, 4:16, :, 1, :], in0=spread(stab[:, 4:16, 0:16], 12, 16),
+            scalar1=-1.0, scalar2=0.0, op0=ALU.mult, op1=ALU.add,
+        )
+
+        def table_part(gp):
+            pt = pst.tile([P, 2, T, P], BF16, name="pt", tag="t")
+            for tab in range(2):
+                for t in range(T):
+                    nc.tensor.transpose(pt[:, tab, t, :], csrep[:, tab, T * gp + t, :], ident_b[:])
+            nc.scalar.copy(
+                out=csT[:, :, 512 * gp : 512 * (gp + 1)], in_=pt[:].rearrange("p b t c -> p b (t c)")
+            )
+
+        bias_bc = const.tile([P, 1024], F32, name="bias_bc")
+        for k in range(2):
+            nc.scalar.copy(out=bias_bc[:, 512 * k : 512 * (k + 1)], in_=pbs[k][:])
+        x_transposes(0)
+        x_copy_out(0)
+        table_part(0)
+
+        wg = const.tile([P, 3 * E, 4], BF16, name="wg", align_bytes=64)
+        wc = const.tile([P, 3 * E], U32, name="wc", align_bytes=64)
+        ws = const.tile([P, 3 * E], U8, name="ws", align_bytes=64)
+
+        def w_quantise(c0):
+            nc.vector.quantize_mx(
+                out=wc[:, c0 : c0 + 512].bitcast(FP8X4),
+                scales=ws[:, c0 : c0 + 512],
+                in_=wg[:, c0 : c0 + 512, :].rearrange("q c t -> q (c t)"),
+            )
+
+        nc.vector.tensor_copy(
+            out=wg[:, VAL : VAL + 512, :].rearrange("q (c i) t -> q c t i", i=4),
+            in_=wraw[:, :, 1024:1536].rearrange("q t (c i) -> q c t i", i=4),
+        )
+        biasT = const.tile([P, 4], F32, name="biasT")
+        nc.vector.tensor_copy(
+            out=biasT[:], in_=pbt[:, 0:128].rearrange("p (i n) -> p i n", n=32)[:, :, 0]
+        )
+        w_quantise(VAL)
+        x_quantise(0)
+        wqk = wraw[:, :, 0:1024].rearrange("q t (g w j) -> q w g j t", g=16, w=2)
+        for hf in range(2):
+            gs = slice(8 * hf, 8 * (hf + 1))
+            nc.vector.tensor_copy(
+                out=wg[:, ROT + 256 * hf : ROT + 256 * (hf + 1), :].rearrange("q (g j) t -> q g j t", g=8),
+                in_=wqk[:, 0, gs],
+            )
+            nc.scalar.copy(
+                out=wg[:, PAS + 256 * hf : PAS + 256 * (hf + 1), :].rearrange("q (g j) t -> q g j t", g=8),
+                in_=wqk[:, 1, gs],
+            )
+        w_quantise(ROT)
+        w_quantise(PAS)
+
+        oqk = {}
+        ovs = {}
+        mw = {}
+
+        def mx(out, lhsT, lhsT_scale, rhs, rhs_scale):
+            nc.tensor.matmul_mx(
+                out=out, lhsT=lhsT.bitcast(FP8X4), lhsT_scale=lhsT_scale,
+                rhs=rhs.bitcast(FP8X4), rhs_scale=rhs_scale, start=True, stop=True,
+            )
+
+        def rot_block(g, i):
+            bank = psr.tile([P, 512], F32, name="rbank", tag="r")
+            cols = slice(ROT + P * i, ROT + P * (i + 1))
+            mx(bank[:], wc[:, cols], ws[:, cols], xc[g][:], xs[g][:])
+            m = mwp.tile([P, 2, 512], F32, name="mw%d" % i, tag="mw%d" % i)
+            gp = g % 4
+            nc.vector.scalar_tensor_tensor(
+                out=m[:],
+                in0=bank[:].unsqueeze(1).to_broadcast([P, 2, 512]),
+                scalar=biasT[:, i : i + 1],
+                in1=csT[:, :, 512 * gp : 512 * (gp + 1)],
+                op0=ALU.add,
+                op1=ALU.mult,
+            )
+            mw[(g, i)] = m
+
+        def token_bank(g, t, c0):
+            bank = psa.tile([P, 512], F32, name="abank", tag="a")
+            cols = slice(P * t, P * (t + 1))
+            mx(bank[:], xc[g][:, cols], xs[g][:, cols], wc[:, c0 : c0 + 512], ws[:, c0 : c0 + 512])
+            return bank
+
+        def out_rows(q, g, t0):
+            return outs[q][512 * g : 512 * (g + 1), :].rearrange("(p t) c -> p t c", t=T)[:, t0 : t0 + 2, :]
+
+        def value_tile(g, t):
+            if t == 0:
+                ovs[g] = ovp.tile([P, T, 512], F32, name="ov", tag="ov")
+            bank = token_bank(g, t, VAL)
+            nc.scalar.copy(out=ovs[g][:, t, :], in_=bank[:])
+
+        def value_finish(g, t0):
+            ov = ovs[g][:, t0 : t0 + 2, :]
+            nc.gpsimd.tensor_tensor(
+                out=ov, in0=ov, in1=bias_bc[:, 512:1024].unsqueeze(1).to_broadcast([P, 2, 512]), op=ALU.add
+            )
+            nc.sync.dma_start(out=out_rows(2, g, t0), in_=ov)
+
+        def pass_tile(g, t):
+            if t == 0:
+                oqk[g] = oqkp.tile([P, 2, T, 512], F32, name="oqk", tag="oqk")
+            bank = token_bank(g, t, PAS)
+            bv = bank[:].rearrange("p (q h j) -> p q h j", q=2, h=8)
+            dst = oqk[g][:, :, t, :].rearrange("p q (h d) -> p q h d", d=64)[:, :, :, 32:64]
+            if t >= 2:
+                bn = bias_bc[:, 0:512].rearrange("p (q h j) -> p q h j", q=2, h=8)
+                nc.vector.tensor_tensor(out=dst, in0=bv, in1=bn, op=ALU.add)
+            else:
+                nc.scalar.copy(out=dst, in_=bv)
+
+        def pass_finish(g):
+            dst = oqk[g][:, :, 0:2, :].rearrange("p q t (h d) -> p q t h d", d=64)[:, :, :, :, 32:64]
+            nc.gpsimd.tensor_tensor(
+                out=dst, in0=dst,
+                in1=bias_bc[:, 0:512].rearrange("p (q o h j) -> p q o h j", q=2, o=1, h=8).to_broadcast([P, 2, 2, 8, 32]),
+                op=ALU.add,
+            )
+
+        def back_tile(g, t):
+            bt = pst.tile([P, 512], F32, name="bt", tag="t")
+            for i in range(4):
+                for part, moving in ((0, ident_f), (1, perm_f)):
+                    nc.tensor.matmul(
+                        bt[:, P * i : P * (i + 1)],
+                        lhsT=mw[(g, i)][:, part, P * t : P * (t + 1)], rhs=moving[:],
+                        is_transpose=True, start=(part == 0), stop=(part == 1),
+                    )
+            nc.scalar.copy(
+                out=oqk[g][:, :, t, :].rearrange("p q (h d) -> p q h d", d=64)[:, :, :, 0:32],
+                in_=bt[:].rearrange("p (q h j) -> p q h j", q=2, h=8),
+            )
+
+        def store_qk(g, t0):
+            for q in range(2):
+                nc.sync.dma_start(out=out_rows(q, g, t0), in_=oqk[g][:, q, t0 : t0 + 2, :])
+
+        for g in range(GROUPS + 1):
+            work = g < GROUPS
+            nxt = g + 1 < GROUPS
+            if g == 0:
+                value_tile(g, 0)
+                value_tile(g, 1)
+                rot_block(g, 0)
+                rot_block(g, 1)
+            elif work:
+                rot_block(g, 0)
+                rot_block(g, 1)
+                value_tile(g, 0)
+                value_tile(g, 1)
+            if work:
+                value_finish(g, 0)
+            if nxt:
+                x_transposes(g + 1)
+                x_copy_out(g + 1)
+            if g == 0:
+                table_part(1)
+            else:
+                back_tile(g - 1, 0)
+
+            if work:
+                rot_block(g, 2)
+                value_tile(g, 2)
+                value_tile(g, 3)
+                value_finish(g, 2)
+                pass_tile(g, 0)
+            if nxt:
+                x_quantise(g + 1)
+            if g == 0:
+                table_part(2)
+                table_part(3)
+            else:
+                back_tile(g - 1, 1)
+                store_qk(g - 1, 0)
+                back_tile(g - 1, 2)
+
+            if work:
+                rot_block(g, 3)
+                pass_tile(g, 1)
+                pass_finish(g)
+                pass_tile(g, 2)
+                pass_tile(g, 3)
+            if g > 0:
+                back_tile(g - 1, 3)
+                store_qk(g - 1, 2)

@@ -42,15 +42,17 @@ def tile_improvedattention_pa_t_kernel(
         ctx.enter_context(tc.manual_schedule())
 
         bnat = const.tile([P, 3 * E], BF16, name="bnat")
-        nc.vector.memset(bnat[:], 0.0)
+        nc.vector.memset(bnat[:].bitcast(U32), 0)
         ctab = const.tile([P, 16, 32], BF16, name="ctab")
         stab = const.tile([P, 16, 32], BF16, name="stab")
-        nc.scalar.dma_start(out=bnat[0:1, :], in_=b_qkv.rearrange("(o c) -> o c", o=1))
-        for tab_sb, tab in ((stab, sin_tab), (ctab, cos_tab)):
-            nc.scalar.dma_start(
-                out=tab_sb[:].rearrange("p (g t) j -> p g (t j)", g=4),
-                in_=tab.rearrange("(g p t) j -> p g (t j)", g=4, p=P, t=T),
-            )
+
+        def load_tables():
+            nc.sync.dma_start(out=bnat[0:1, :], in_=b_qkv.rearrange("(o c) -> o c", o=1))
+            for tab_sb, tab in ((stab, sin_tab), (ctab, cos_tab)):
+                nc.sync.dma_start(
+                    out=tab_sb[:].rearrange("p (g t) j -> p g (t j)", g=4),
+                    in_=tab.rearrange("(g p t) j -> p g (t j)", g=4, p=P, t=T),
+                )
 
         x_sb = []
         for g in range(GROUPS):
@@ -70,8 +72,12 @@ def tile_improvedattention_pa_t_kernel(
                 in_=W_qkv[:, c0 : c0 + 512].rearrange("(q t) c -> q t c", t=4),
             )
 
-        load_x(0)
+        x0 = xf[0:512, :].rearrange("(p t) k -> p (t k)", t=T)
+        for hf in range(2):
+            cols = slice(2 * E * hf, 2 * E * (hf + 1))
+            nc.sync.dma_start(out=x_sb[0][:, cols], in_=x0[:, cols])
         load_w(1024)
+        load_tables()
         load_w(0)
         load_w(512)
         for g in range(1, GROUPS):
@@ -125,6 +131,9 @@ def tile_improvedattention_pa_t_kernel(
             xc[g] = codes
             xs[g] = scales
 
+        x_transposes(0)
+        x_copy_out(0)
+
         brow = const.tile([P, 1024], BF16, name="brow")
         bqk = bnat[:, 0:1024].rearrange("p (g w j) -> p w g j", g=16, w=2)
         nc.vector.tensor_copy(out=brow[:, 512:1024].rearrange("p (g j) -> p g j", g=16), in_=bqk[:, 1])
@@ -177,10 +186,8 @@ def tile_improvedattention_pa_t_kernel(
             )
 
         bias_bc = const.tile([P, 1024], F32, name="bias_bc")
-        for k in range(2):
+        for k in (1, 0):
             nc.scalar.copy(out=bias_bc[:, 512 * k : 512 * (k + 1)], in_=pbs[k][:])
-        x_transposes(0)
-        x_copy_out(0)
         table_part(0)
 
         wg = const.tile([P, 3 * E, 4], BF16, name="wg", align_bytes=64)

@@ -35,9 +35,8 @@ def tile_improvedattention_pa_t_kernel(
         mwp = ctx.enter_context(tc.tile_pool(name="mwp", bufs=2))
         oqkp = ctx.enter_context(tc.tile_pool(name="oqkp", bufs=3))
         ovp = ctx.enter_context(tc.tile_pool(name="ovp", bufs=3))
-        psr = ctx.enter_context(tc.psum_pool(name="psr", bufs=2))
-        psa = ctx.enter_context(tc.psum_pool(name="psa", bufs=3))
-        pst = ctx.enter_context(tc.psum_pool(name="pst", bufs=3))
+        psv = ctx.enter_context(tc.psum_pool(name="psv", bufs=4))
+        pss = ctx.enter_context(tc.psum_pool(name="pss", bufs=4))
         ctx.enter_context(nc.allow_non_contiguous_dma(reason="short rows of tables and column chunks"))
         ctx.enter_context(tc.manual_schedule())
 
@@ -64,22 +63,24 @@ def tile_improvedattention_pa_t_kernel(
                 in_=xf[512 * g : 512 * (g + 1), :].rearrange("(p t) k -> p (t k)", t=T),
             )
 
-        wraw = const.tile([P, 4, 3 * E], BF16, name="wraw")
+        wraw = []
+        for n in range(3):
+            wraw.append(const.tile([P, 4, 512], BF16, name="wraw%d" % n))
 
-        def load_w(c0):
+        def load_w(n):
             nc.sync.dma_start(
-                out=wraw[:, :, c0 : c0 + 512],
-                in_=W_qkv[:, c0 : c0 + 512].rearrange("(q t) c -> q t c", t=4),
+                out=wraw[n][:],
+                in_=W_qkv[:, 512 * n : 512 * (n + 1)].rearrange("(q t) c -> q t c", t=4),
             )
 
         x0 = xf[0:512, :].rearrange("(p t) k -> p (t k)", t=T)
         for hf in range(2):
             cols = slice(2 * E * hf, 2 * E * (hf + 1))
             nc.sync.dma_start(out=x_sb[0][:, cols], in_=x0[:, cols])
-        load_w(1024)
+        load_w(2)
         load_tables()
         load_w(0)
-        load_w(512)
+        load_w(1)
         for g in range(1, GROUPS):
             load_x(g)
 
@@ -101,10 +102,12 @@ def tile_improvedattention_pa_t_kernel(
         xgrouped = {}
 
         def x_transposes(g):
+            if g >= GROUPS:
+                return
             xw = x_sb[g][:].bitcast(F32)
             banks = []
             for hf in range(2):
-                xt = pst.tile([P, 4, P], F32, name="xt", tag="t")
+                xt = pss.tile([P, 4, P], F32, name="xt", tag="s")
                 for tt in range(2):
                     for u in range(2):
                         c0 = 256 * (2 * hf + tt)
@@ -113,6 +116,8 @@ def tile_improvedattention_pa_t_kernel(
             xbanks[g] = banks
 
         def x_copy_out(g):
+            if g >= GROUPS:
+                return
             grouped = xgr.tile([P, 4 * 512], BF16, name="grouped", tag="grouped", align_bytes=64)
             g32 = grouped[:].bitcast(F32)
             for hf in range(2):
@@ -125,6 +130,8 @@ def tile_improvedattention_pa_t_kernel(
             xgrouped[g] = grouped
 
         def x_quantise(g):
+            if g >= GROUPS:
+                return
             codes = xq.tile([P, 512], U32, name="xcodes", tag="xcodes", align_bytes=64)
             scales = xq.tile([P, 512], U8, name="xscales", tag="xscales", align_bytes=64)
             nc.vector.quantize_mx(out=codes[:].bitcast(FP8X4), scales=scales[:], in_=xgrouped[g][:])
@@ -140,10 +147,10 @@ def tile_improvedattention_pa_t_kernel(
         nc.vector.tensor_copy(out=brow[:, 0:512].rearrange("p (g j) -> p g j", g=16), in_=bqk[:, 0])
         pbs = []
         for rhs in (brow[:, 512:1024], bnat[:, 1024:1536]):
-            pb = psa.tile([P, 512], F32, name="pb", tag="a")
+            pb = psv.tile([P, 512], F32, name="pb", tag="v")
             nc.tensor.matmul(pb[:], lhsT=ones_b[:], rhs=rhs, start=True, stop=True)
             pbs.append(pb)
-        pbt = psa.tile([P, 512], F32, name="pbt", tag="a")
+        pbt = psv.tile([P, 512], F32, name="pbt", tag="v")
         for i in range(4):
             nc.tensor.matmul(
                 pbt[:, 32 * i : 32 * (i + 1)], lhsT=brow[:, P * i : P * (i + 1)], rhs=ones_b[:, 0:32],
@@ -177,7 +184,7 @@ def tile_improvedattention_pa_t_kernel(
         )
 
         def table_part(gp):
-            pt = pst.tile([P, 2, T, P], BF16, name="pt", tag="t")
+            pt = pss.tile([P, 2, T, P], BF16, name="pt", tag="s")
             for tab in range(2):
                 for t in range(T):
                     nc.tensor.transpose(pt[:, tab, t, :], csrep[:, tab, T * gp + t, :], ident_b[:])
@@ -203,7 +210,7 @@ def tile_improvedattention_pa_t_kernel(
 
         nc.vector.tensor_copy(
             out=wg[:, VAL : VAL + 512, :].rearrange("q (c i) t -> q c t i", i=4),
-            in_=wraw[:, :, 1024:1536].rearrange("q t (c i) -> q c t i", i=4),
+            in_=wraw[2][:].rearrange("q t (c i) -> q c t i", i=4),
         )
         biasT = const.tile([P, 4], F32, name="biasT")
         nc.vector.tensor_copy(
@@ -211,16 +218,15 @@ def tile_improvedattention_pa_t_kernel(
         )
         w_quantise(VAL)
         x_quantise(0)
-        wqk = wraw[:, :, 0:1024].rearrange("q t (g w j) -> q w g j t", g=16, w=2)
         for hf in range(2):
-            gs = slice(8 * hf, 8 * (hf + 1))
+            wqk = wraw[hf][:].rearrange("q t (g w j) -> q w g j t", g=8, w=2)
             nc.vector.tensor_copy(
                 out=wg[:, ROT + 256 * hf : ROT + 256 * (hf + 1), :].rearrange("q (g j) t -> q g j t", g=8),
-                in_=wqk[:, 0, gs],
+                in_=wqk[:, 0],
             )
             nc.scalar.copy(
                 out=wg[:, PAS + 256 * hf : PAS + 256 * (hf + 1), :].rearrange("q (g j) t -> q g j t", g=8),
-                in_=wqk[:, 1, gs],
+                in_=wqk[:, 1],
             )
         w_quantise(ROT)
         w_quantise(PAS)
@@ -228,6 +234,7 @@ def tile_improvedattention_pa_t_kernel(
         oqk = {}
         ovs = {}
         mw = {}
+        banks = {}
 
         def mx(out, lhsT, lhsT_scale, rhs, rhs_scale):
             nc.tensor.matmul_mx(
@@ -235,15 +242,20 @@ def tile_improvedattention_pa_t_kernel(
                 rhs=rhs.bitcast(FP8X4), rhs_scale=rhs_scale, start=True, stop=True,
             )
 
-        def rot_block(g, i):
-            bank = psr.tile([P, 512], F32, name="rbank", tag="r")
+        def turn_mm(g, i):
+            if g >= GROUPS:
+                return
+            bank = psv.tile([P, 512], F32, name="rbank", tag="v")
             cols = slice(ROT + P * i, ROT + P * (i + 1))
             mx(bank[:], wc[:, cols], ws[:, cols], xc[g][:], xs[g][:])
+            banks["turn", g, i] = bank
+
+        def turn(g, i):
             m = mwp.tile([P, 2, 512], F32, name="mw%d" % i, tag="mw%d" % i)
             gp = g % 4
             nc.vector.scalar_tensor_tensor(
                 out=m[:],
-                in0=bank[:].unsqueeze(1).to_broadcast([P, 2, 512]),
+                in0=banks["turn", g, i][:].unsqueeze(1).to_broadcast([P, 2, 512]),
                 scalar=biasT[:, i : i + 1],
                 in1=csT[:, :, 512 * gp : 512 * (gp + 1)],
                 op0=ALU.add,
@@ -251,50 +263,50 @@ def tile_improvedattention_pa_t_kernel(
             )
             mw[(g, i)] = m
 
-        def token_bank(g, t, c0):
-            bank = psa.tile([P, 512], F32, name="abank", tag="a")
+        def token_mm(kind, g, t, on_vector):
+            if on_vector:
+                bank = psv.tile([P, 512], F32, name="vbank", tag="v")
+            else:
+                bank = pss.tile([P, 512], F32, name="sbank", tag="s")
+            c0 = VAL if kind == "val" else PAS
             cols = slice(P * t, P * (t + 1))
             mx(bank[:], xc[g][:, cols], xs[g][:, cols], wc[:, c0 : c0 + 512], ws[:, c0 : c0 + 512])
-            return bank
+            banks[kind, g, t] = bank
 
         def out_rows(q, g, t0):
             return outs[q][512 * g : 512 * (g + 1), :].rearrange("(p t) c -> p t c", t=T)[:, t0 : t0 + 2, :]
 
-        def value_tile(g, t):
+        def val_out(g, t):
             if t == 0:
                 ovs[g] = ovp.tile([P, T, 512], F32, name="ov", tag="ov")
-            bank = token_bank(g, t, VAL)
-            nc.scalar.copy(out=ovs[g][:, t, :], in_=bank[:])
+            nc.scalar.copy(out=ovs[g][:, t, :], in_=banks["val", g, t][:])
 
-        def value_finish(g, t0):
+        def val_finish(g, t0):
             ov = ovs[g][:, t0 : t0 + 2, :]
             nc.gpsimd.tensor_tensor(
                 out=ov, in0=ov, in1=bias_bc[:, 512:1024].unsqueeze(1).to_broadcast([P, 2, 512]), op=ALU.add
             )
             nc.sync.dma_start(out=out_rows(2, g, t0), in_=ov)
 
-        def pass_tile(g, t):
-            if t == 0:
-                oqk[g] = oqkp.tile([P, 2, T, 512], F32, name="oqk", tag="oqk")
-            bank = token_bank(g, t, PAS)
-            bv = bank[:].rearrange("p (q h j) -> p q h j", q=2, h=8)
-            dst = oqk[g][:, :, t, :].rearrange("p q (h d) -> p q h d", d=64)[:, :, :, 32:64]
-            if t >= 2:
-                bn = bias_bc[:, 0:512].rearrange("p (q h j) -> p q h j", q=2, h=8)
-                nc.vector.tensor_tensor(out=dst, in0=bv, in1=bn, op=ALU.add)
-            else:
-                nc.scalar.copy(out=dst, in_=bv)
+        pass_bias = bias_bc[:, 0:512].rearrange("p (q h j) -> p q h j", q=2, h=8)
 
-        def pass_finish(g):
-            dst = oqk[g][:, :, 0:2, :].rearrange("p q t (h d) -> p q t h d", d=64)[:, :, :, :, 32:64]
-            nc.gpsimd.tensor_tensor(
-                out=dst, in0=dst,
-                in1=bias_bc[:, 0:512].rearrange("p (q o h j) -> p q o h j", q=2, o=1, h=8).to_broadcast([P, 2, 2, 8, 32]),
-                op=ALU.add,
-            )
+        def half(g, t, c0):
+            return oqk[g][:, :, t, :].rearrange("p q (h d) -> p q h d", d=64)[:, :, :, c0 : c0 + 32]
+
+        def pass_out(g, t, on_vector):
+            if g not in oqk:
+                oqk[g] = oqkp.tile([P, 2, T, 512], F32, name="oqk", tag="oqk")
+            bv = banks["pass", g, t][:].rearrange("p (q h j) -> p q h j", q=2, h=8)
+            if on_vector:
+                nc.vector.tensor_tensor(out=half(g, t, 32), in0=bv, in1=pass_bias, op=ALU.add)
+            else:
+                nc.scalar.copy(out=half(g, t, 32), in_=bv)
+
+        def pass_finish(g, t):
+            nc.gpsimd.tensor_tensor(out=half(g, t, 32), in0=half(g, t, 32), in1=pass_bias, op=ALU.add)
 
         def back_tile(g, t):
-            bt = pst.tile([P, 512], F32, name="bt", tag="t")
+            bt = pss.tile([P, 512], F32, name="bt", tag="s")
             for i in range(4):
                 for part, moving in ((0, ident_f), (1, perm_f)):
                     nc.tensor.matmul(
@@ -302,60 +314,77 @@ def tile_improvedattention_pa_t_kernel(
                         lhsT=mw[(g, i)][:, part, P * t : P * (t + 1)], rhs=moving[:],
                         is_transpose=True, start=(part == 0), stop=(part == 1),
                     )
-            nc.scalar.copy(
-                out=oqk[g][:, :, t, :].rearrange("p q (h d) -> p q h d", d=64)[:, :, :, 0:32],
-                in_=bt[:].rearrange("p (q h j) -> p q h j", q=2, h=8),
-            )
+            nc.scalar.copy(out=half(g, t, 0), in_=bt[:].rearrange("p (q h j) -> p q h j", q=2, h=8))
 
         def store_qk(g, t0):
             for q in range(2):
                 nc.sync.dma_start(out=out_rows(q, g, t0), in_=oqk[g][:, q, t0 : t0 + 2, :])
 
-        for g in range(GROUPS + 1):
-            work = g < GROUPS
-            nxt = g + 1 < GROUPS
-            if g == 0:
-                value_tile(g, 0)
-                value_tile(g, 1)
-                rot_block(g, 0)
-                rot_block(g, 1)
-            elif work:
-                rot_block(g, 0)
-                rot_block(g, 1)
-                value_tile(g, 0)
-                value_tile(g, 1)
-            if work:
-                value_finish(g, 0)
-            if nxt:
-                x_transposes(g + 1)
-                x_copy_out(g + 1)
-            if g == 0:
-                table_part(1)
-            else:
-                back_tile(g - 1, 0)
+        def val_tile(g, t):
+            token_mm("val", g, t, False)
+            val_out(g, t)
 
-            if work:
-                rot_block(g, 2)
-                value_tile(g, 2)
-                value_tile(g, 3)
-                value_finish(g, 2)
-                pass_tile(g, 0)
-            if nxt:
-                x_quantise(g + 1)
-            if g == 0:
-                table_part(2)
-                table_part(3)
-            else:
-                back_tile(g - 1, 1)
-                store_qk(g - 1, 0)
-                back_tile(g - 1, 2)
+        def round_end(g):
+            token_mm("pass", g, 3, True)
+            pass_out(g, 2, True)
+            turn_mm(g + 1, 0)
+            turn_mm(g + 1, 1)
+            pass_out(g, 3, True)
+            for t in range(T):
+                back_tile(g, t)
+                if t % 2 == 1:
+                    store_qk(g, t - 1)
 
-            if work:
-                rot_block(g, 3)
-                pass_tile(g, 1)
-                pass_finish(g)
-                pass_tile(g, 2)
-                pass_tile(g, 3)
-            if g > 0:
-                back_tile(g - 1, 3)
-                store_qk(g - 1, 2)
+        val_tile(0, 0)
+        val_tile(0, 1)
+        val_finish(0, 0)
+        val_tile(0, 2)
+        turn_mm(0, 0)
+        turn_mm(0, 1)
+        val_tile(0, 3)
+        val_finish(0, 2)
+        turn_mm(0, 2)
+        turn(0, 0)
+        turn_mm(0, 3)
+        turn(0, 1)
+        x_transposes(1)
+        x_copy_out(1)
+        table_part(1)
+        token_mm("pass", 0, 1, True)
+        turn(0, 2)
+        token_mm("pass", 0, 2, True)
+        turn(0, 3)
+        x_quantise(1)
+        token_mm("pass", 0, 0, False)
+        pass_out(0, 0, False)
+        pass_finish(0, 0)
+        pass_out(0, 1, True)
+        x_transposes(2)
+        x_copy_out(2)
+        round_end(0)
+        table_part(2)
+        table_part(3)
+
+        for g in range(1, GROUPS):
+            turn_mm(g, 2)
+            turn(g, 0)
+            x_quantise(g + 1)
+            val_tile(g, 0)
+            turn_mm(g, 3)
+            turn(g, 1)
+            val_tile(g, 1)
+            val_finish(g, 0)
+            val_tile(g, 2)
+            token_mm("pass", g, 1, True)
+            turn(g, 2)
+            val_tile(g, 3)
+            val_finish(g, 2)
+            token_mm("pass", g, 2, True)
+            turn(g, 3)
+            x_transposes(g + 2)
+            x_copy_out(g + 2)
+            token_mm("pass", g, 0, False)
+            pass_out(g, 0, False)
+            pass_finish(g, 0)
+            pass_out(g, 1, True)
+            round_end(g)

@@ -15,6 +15,8 @@ TOKENS = 4096
 E = 512
 GROUPS = 8
 T = 4
+STEPS = 16
+N = 256
 FLOPS = 2 * TOKENS * E * 3 * E
 
 ROT, PAS, VAL = 0, 512, 1024
@@ -30,11 +32,12 @@ def tile_improvedattention_pa_t_kernel(
     with ExitStack() as ctx:
         const = ctx.enter_context(tc.tile_pool(name="const", bufs=1))
         xin = ctx.enter_context(tc.tile_pool(name="xin", bufs=GROUPS))
-        xgr = ctx.enter_context(tc.tile_pool(name="xgr", bufs=2))
-        xq = ctx.enter_context(tc.tile_pool(name="xq", bufs=3))
-        mwp = ctx.enter_context(tc.tile_pool(name="mwp", bufs=2))
-        oqkp = ctx.enter_context(tc.tile_pool(name="oqkp", bufs=3))
-        ovp = ctx.enter_context(tc.tile_pool(name="ovp", bufs=3))
+        xpp = ctx.enter_context(tc.tile_pool(name="xpp", bufs=2))
+        xgr = ctx.enter_context(tc.tile_pool(name="xgr", bufs=3))
+        xq = ctx.enter_context(tc.tile_pool(name="xq", bufs=5))
+        mwp = ctx.enter_context(tc.tile_pool(name="mwp", bufs=3))
+        oqkp = ctx.enter_context(tc.tile_pool(name="oqkp", bufs=6))
+        ovp = ctx.enter_context(tc.tile_pool(name="ovp", bufs=6))
         psv = ctx.enter_context(tc.psum_pool(name="psv", bufs=4))
         pss = ctx.enter_context(tc.psum_pool(name="pss", bufs=4))
         ctx.enter_context(nc.allow_non_contiguous_dma(reason="short rows of tables and column chunks"))
@@ -45,27 +48,15 @@ def tile_improvedattention_pa_t_kernel(
         ctab = const.tile([P, 16, 32], BF16, name="ctab")
         stab = const.tile([P, 16, 32], BF16, name="stab")
 
-        def load_tables():
-            nc.sync.dma_start(out=bnat[0:1, :], in_=b_qkv.rearrange("(o c) -> o c", o=1))
-            for tab_sb, tab in ((stab, sin_tab), (ctab, cos_tab)):
-                nc.sync.dma_start(
-                    out=tab_sb[:].rearrange("p (g t) j -> p g (t j)", g=4),
-                    in_=tab.rearrange("(g p t) j -> p g (t j)", g=4, p=P, t=T),
-                )
-
         x_sb = []
         for g in range(GROUPS):
             x_sb.append(xin.tile([P, T * E], BF16, name="x_sb%d" % g, tag="x_sb"))
-
-        def load_x(g):
-            nc.sync.dma_start(
-                out=x_sb[g][:],
-                in_=xf[512 * g : 512 * (g + 1), :].rearrange("(p t) k -> p (t k)", t=T),
-            )
-
         wraw = []
         for n in range(3):
             wraw.append(const.tile([P, 4, 512], BF16, name="wraw%d" % n))
+
+        def x_rows(g):
+            return xf[512 * g : 512 * (g + 1), :].rearrange("(p t) k -> p (t k)", t=T)
 
         def load_w(n):
             nc.sync.dma_start(
@@ -73,16 +64,21 @@ def tile_improvedattention_pa_t_kernel(
                 in_=W_qkv[:, 512 * n : 512 * (n + 1)].rearrange("(q t) c -> q t c", t=4),
             )
 
-        x0 = xf[0:512, :].rearrange("(p t) k -> p (t k)", t=T)
         for hf in range(2):
             cols = slice(2 * E * hf, 2 * E * (hf + 1))
-            nc.sync.dma_start(out=x_sb[0][:, cols], in_=x0[:, cols])
-        load_w(2)
-        load_tables()
+            nc.sync.dma_start(out=x_sb[0][:, cols], in_=x_rows(0)[:, cols])
+            if hf == 0:
+                load_w(2)
+                nc.sync.dma_start(out=bnat[0:1, :], in_=b_qkv.rearrange("(o c) -> o c", o=1))
+        for tab_sb, tab in ((stab, sin_tab), (ctab, cos_tab)):
+            nc.sync.dma_start(
+                out=tab_sb[:].rearrange("p (g t) j -> p g (t j)", g=4),
+                in_=tab.rearrange("(g p t) j -> p g (t j)", g=4, p=P, t=T),
+            )
         load_w(0)
         load_w(1)
         for g in range(1, GROUPS):
-            load_x(g)
+            nc.sync.dma_start(out=x_sb[g][:], in_=x_rows(g))
 
         ident_f = const.tile([P, P], F32, name="ident_f")
         make_identity(nc, ident_f[:])
@@ -98,108 +94,88 @@ def tile_improvedattention_pa_t_kernel(
 
         xc = {}
         xs = {}
+        xperm = {}
         xbanks = {}
         xgrouped = {}
 
-        def x_transposes(g):
-            if g >= GROUPS:
-                return
-            xw = x_sb[g][:].bitcast(F32)
-            banks = []
-            for hf in range(2):
+        def x_words(s):
+            return x_sb[s // 2][:].bitcast(F32)[:, 512 * (s % 2) : 512 * (s % 2 + 1)]
+
+        def x_split(s):
+            if s < STEPS:
+                xperm[s] = xpp.tile([P, 2, 2, P], F32, name="xperm", tag="xperm")
+                nc.scalar.copy(
+                    out=xperm[s][:], in_=x_words(s).rearrange("p (t w u) -> p t u w", t=2, u=2)
+                )
+
+        def x_transposes(s):
+            if s < STEPS:
                 xt = pss.tile([P, 4, P], F32, name="xt", tag="s")
                 for tt in range(2):
                     for u in range(2):
-                        c0 = 256 * (2 * hf + tt)
-                        nc.tensor.transpose(xt[:, 2 * tt + u, :], xw[:, c0 + u : c0 + 256 : 2], ident_f[:])
-                banks.append(xt)
-            xbanks[g] = banks
+                        if s in xperm:
+                            src = xperm[s][:, tt, u, :]
+                        else:
+                            src = x_words(s)[:, 256 * tt + u : 256 * (tt + 1) : 2]
+                        nc.tensor.transpose(xt[:, 2 * tt + u, :], src, ident_f[:])
+                xbanks[s] = xt
 
-        def x_copy_out(g):
-            if g >= GROUPS:
-                return
-            grouped = xgr.tile([P, 4 * 512], BF16, name="grouped", tag="grouped", align_bytes=64)
-            g32 = grouped[:].bitcast(F32)
-            for hf in range(2):
+        def x_copy_out(s):
+            if s < STEPS:
+                xgrouped[s] = xgr.tile([P, 4 * N], BF16, name="grouped", tag="grouped", align_bytes=64)
                 nc.scalar.copy(
-                    out=g32[:, 512 * hf : 512 * (hf + 1)].rearrange(
-                        "q (tt p u) -> q tt p u", tt=2, p=P, u=2
-                    ),
-                    in_=xbanks[g][hf][:].rearrange("q (tt u) p -> q tt p u", tt=2, u=2),
+                    out=xgrouped[s][:].bitcast(F32).rearrange("q (tt p u) -> q tt p u", tt=2, p=P, u=2),
+                    in_=xbanks[s][:].rearrange("q (tt u) p -> q tt p u", tt=2, u=2),
                 )
-            xgrouped[g] = grouped
 
-        def x_quantise(g):
-            if g >= GROUPS:
-                return
-            codes = xq.tile([P, 512], U32, name="xcodes", tag="xcodes", align_bytes=64)
-            scales = xq.tile([P, 512], U8, name="xscales", tag="xscales", align_bytes=64)
-            nc.vector.quantize_mx(out=codes[:].bitcast(FP8X4), scales=scales[:], in_=xgrouped[g][:])
-            xc[g] = codes
-            xs[g] = scales
-
-        x_transposes(0)
-        x_copy_out(0)
+        def x_quantise(s):
+            if s < STEPS:
+                xc[s] = xq.tile([P, N], U32, name="xcodes", tag="xcodes", align_bytes=64)
+                xs[s] = xq.tile([P, N], U8, name="xscales", tag="xscales", align_bytes=64)
+                nc.vector.quantize_mx(out=xc[s][:].bitcast(FP8X4), scales=xs[s][:], in_=xgrouped[s][:])
 
         brow = const.tile([P, 1024], BF16, name="brow")
-        bqk = bnat[:, 0:1024].rearrange("p (g w j) -> p w g j", g=16, w=2)
-        nc.vector.tensor_copy(out=brow[:, 512:1024].rearrange("p (g j) -> p g j", g=16), in_=bqk[:, 1])
-        nc.vector.tensor_copy(out=brow[:, 0:512].rearrange("p (g j) -> p g j", g=16), in_=bqk[:, 0])
-        pbs = []
-        for rhs in (brow[:, 512:1024], bnat[:, 1024:1536]):
-            pb = psv.tile([P, 512], F32, name="pb", tag="v")
-            nc.tensor.matmul(pb[:], lhsT=ones_b[:], rhs=rhs, start=True, stop=True)
-            pbs.append(pb)
-        pbt = psv.tile([P, 512], F32, name="pbt", tag="v")
-        for i in range(4):
-            nc.tensor.matmul(
-                pbt[:, 32 * i : 32 * (i + 1)], lhsT=brow[:, P * i : P * (i + 1)], rhs=ones_b[:, 0:32],
-                start=True, stop=True,
-            )
-
+        bias_bc = const.tile([P, 1024], F32, name="bias_bc")
+        biasT = const.tile([P, 4], F32, name="biasT")
         csrep = const.tile([P, 2, 16, P], BF16, name="csrep")
-        csT = const.tile([P, 2, 2048], BF16, name="csT")
+        csT = []
+        for gp in range(4):
+            csT.append(const.tile([P, 2, 512], BF16, name="csT%d" % gp))
         crep = csrep[:, 0].rearrange("p a (r j) -> p a r j", r=4)
         srep = csrep[:, 1].rearrange("p a (r w i) -> p a r w i", r=4, w=2)
+        wg = const.tile([P, 3 * E, 4], BF16, name="wg", align_bytes=64)
+        wc = const.tile([P, 3 * E], U32, name="wc", align_bytes=64)
+        ws = const.tile([P, 3 * E], U8, name="ws", align_bytes=64)
+
+        def bias_row_mm(rhs):
+            pb = psv.tile([P, 512], F32, name="pb", tag="v")
+            nc.tensor.matmul(pb[:], lhsT=ones_b[:], rhs=rhs, start=True, stop=True)
+            return pb
 
         def spread(tab_part, n, width):
             return tab_part.unsqueeze(2).to_broadcast([P, n, 4, width])
 
-        nc.vector.tensor_copy(out=srep[:, 0:4, :, 0, :], in_=spread(stab[:, 0:4, 16:32], 4, 16))
-        nc.vector.tensor_scalar_mul(
-            out=srep[:, 0:4, :, 1, :], in0=spread(stab[:, 0:4, 0:16], 4, 16), scalar1=-1.0
-        )
-        nc.scalar.copy(out=crep[:, 0:4], in_=spread(ctab[:, 0:4, :], 4, 32))
-        nc.gpsimd.tensor_scalar(
-            out=crep[:, 4:16], in0=spread(ctab[:, 4:16, :], 12, 32),
-            scalar1=1.0, scalar2=0.0, op0=ALU.mult, op1=ALU.add,
-        )
-        nc.gpsimd.tensor_scalar(
-            out=srep[:, 4:16, :, 0, :], in0=spread(stab[:, 4:16, 16:32], 12, 16),
-            scalar1=1.0, scalar2=0.0, op0=ALU.mult, op1=ALU.add,
-        )
-        nc.gpsimd.tensor_scalar(
-            out=srep[:, 4:16, :, 1, :], in0=spread(stab[:, 4:16, 0:16], 12, 16),
-            scalar1=-1.0, scalar2=0.0, op0=ALU.mult, op1=ALU.add,
-        )
+        def spread_scalar(a0, n):
+            a = slice(a0, a0 + n)
+            nc.scalar.copy(out=crep[:, a], in_=spread(ctab[:, a, :], n, 32))
+            nc.scalar.copy(out=srep[:, a, :, 0, :], in_=spread(stab[:, a, 16:32], n, 16))
+            nc.scalar.mul(out=srep[:, a, :, 1, :], in_=spread(stab[:, a, 0:16], n, 16), mul=-1.0)
+
+        def spread_gpsimd(a0, n):
+            a = slice(a0, a0 + n)
+            for out, src, sign in (
+                (crep[:, a], spread(ctab[:, a, :], n, 32), 1.0),
+                (srep[:, a, :, 0, :], spread(stab[:, a, 16:32], n, 16), 1.0),
+                (srep[:, a, :, 1, :], spread(stab[:, a, 0:16], n, 16), -1.0),
+            ):
+                nc.gpsimd.tensor_scalar(out=out, in0=src, scalar1=sign, scalar2=0.0, op0=ALU.mult, op1=ALU.add)
 
         def table_part(gp):
             pt = pss.tile([P, 2, T, P], BF16, name="pt", tag="s")
             for tab in range(2):
                 for t in range(T):
                     nc.tensor.transpose(pt[:, tab, t, :], csrep[:, tab, T * gp + t, :], ident_b[:])
-            nc.scalar.copy(
-                out=csT[:, :, 512 * gp : 512 * (gp + 1)], in_=pt[:].rearrange("p b t c -> p b (t c)")
-            )
-
-        bias_bc = const.tile([P, 1024], F32, name="bias_bc")
-        for k in (1, 0):
-            nc.scalar.copy(out=bias_bc[:, 512 * k : 512 * (k + 1)], in_=pbs[k][:])
-        table_part(0)
-
-        wg = const.tile([P, 3 * E, 4], BF16, name="wg", align_bytes=64)
-        wc = const.tile([P, 3 * E], U32, name="wc", align_bytes=64)
-        ws = const.tile([P, 3 * E], U8, name="ws", align_bytes=64)
+            nc.scalar.copy(out=csT[gp][:], in_=pt[:].rearrange("p b t c -> p b (t c)"))
 
         def w_quantise(c0):
             nc.vector.quantize_mx(
@@ -208,28 +184,12 @@ def tile_improvedattention_pa_t_kernel(
                 in_=wg[:, c0 : c0 + 512, :].rearrange("q c t -> q (c t)"),
             )
 
-        nc.vector.tensor_copy(
-            out=wg[:, VAL : VAL + 512, :].rearrange("q (c i) t -> q c t i", i=4),
-            in_=wraw[2][:].rearrange("q t (c i) -> q c t i", i=4),
-        )
-        biasT = const.tile([P, 4], F32, name="biasT")
-        nc.vector.tensor_copy(
-            out=biasT[:], in_=pbt[:, 0:128].rearrange("p (i n) -> p i n", n=32)[:, :, 0]
-        )
-        w_quantise(VAL)
-        x_quantise(0)
-        for hf in range(2):
-            wqk = wraw[hf][:].rearrange("q t (g w j) -> q w g j t", g=8, w=2)
-            nc.vector.tensor_copy(
-                out=wg[:, ROT + 256 * hf : ROT + 256 * (hf + 1), :].rearrange("q (g j) t -> q g j t", g=8),
-                in_=wqk[:, 0],
+        def w_half(copy, n, w):
+            c0 = (ROT, PAS)[w] + 256 * n
+            copy(
+                out=wg[:, c0 : c0 + 256, :].rearrange("q (g j) t -> q g j t", g=8),
+                in_=wraw[n][:].rearrange("q t (g w j) -> q w g j t", g=8, w=2)[:, w],
             )
-            nc.scalar.copy(
-                out=wg[:, PAS + 256 * hf : PAS + 256 * (hf + 1), :].rearrange("q (g j) t -> q g j t", g=8),
-                in_=wqk[:, 1],
-            )
-        w_quantise(ROT)
-        w_quantise(PAS)
 
         oqk = {}
         ovs = {}
@@ -242,149 +202,185 @@ def tile_improvedattention_pa_t_kernel(
                 rhs=rhs.bitcast(FP8X4), rhs_scale=rhs_scale, start=True, stop=True,
             )
 
-        def turn_mm(g, i):
-            if g >= GROUPS:
-                return
-            bank = psv.tile([P, 512], F32, name="rbank", tag="v")
-            cols = slice(ROT + P * i, ROT + P * (i + 1))
-            mx(bank[:], wc[:, cols], ws[:, cols], xc[g][:], xs[g][:])
-            banks["turn", g, i] = bank
+        def turn_mm(s, j):
+            if s < STEPS:
+                bank = psv.tile([P, 2, N], F32, name="rbank", tag="v")
+                for e in range(2):
+                    c0 = ROT + P * (2 * j + e)
+                    cols = slice(c0, c0 + P)
+                    mx(bank[:, e, :], wc[:, cols], ws[:, cols], xc[s][:], xs[s][:])
+                banks["turn", s, j] = bank
 
-        def turn(g, i):
-            m = mwp.tile([P, 2, 512], F32, name="mw%d" % i, tag="mw%d" % i)
-            gp = g % 4
+        def turn(s, i):
+            m = mwp.tile([P, 2, N], F32, name="mw%d" % i, tag="mw%d" % i)
+            c0 = N * (s % 2)
             nc.vector.scalar_tensor_tensor(
                 out=m[:],
-                in0=banks["turn", g, i][:].unsqueeze(1).to_broadcast([P, 2, 512]),
+                in0=banks["turn", s, i // 2][:, i % 2, :].unsqueeze(1).to_broadcast([P, 2, N]),
                 scalar=biasT[:, i : i + 1],
-                in1=csT[:, :, 512 * gp : 512 * (gp + 1)],
+                in1=csT[s // 2 % 4][:, :, c0 : c0 + N],
                 op0=ALU.add,
                 op1=ALU.mult,
             )
-            mw[(g, i)] = m
+            mw[s, i] = m
 
-        def token_mm(kind, g, t, on_vector):
-            if on_vector:
-                bank = psv.tile([P, 512], F32, name="vbank", tag="v")
+        def token_mm(kind, s, t):
+            if kind == "val":
+                bank = pss.tile([P, 512], F32, name="vbank", tag="s")
+                c0 = VAL
             else:
-                bank = pss.tile([P, 512], F32, name="sbank", tag="s")
-            c0 = VAL if kind == "val" else PAS
+                bank = psv.tile([P, 512], F32, name="pbank", tag="v")
+                c0 = PAS
             cols = slice(P * t, P * (t + 1))
-            mx(bank[:], xc[g][:, cols], xs[g][:, cols], wc[:, c0 : c0 + 512], ws[:, c0 : c0 + 512])
-            banks[kind, g, t] = bank
+            mx(bank[:], xc[s][:, cols], xs[s][:, cols], wc[:, c0 : c0 + 512], ws[:, c0 : c0 + 512])
+            banks[kind, s, t] = bank
 
-        def out_rows(q, g, t0):
-            return outs[q][512 * g : 512 * (g + 1), :].rearrange("(p t) c -> p t c", t=T)[:, t0 : t0 + 2, :]
+        def out_rows(q, s):
+            g, e = s // 2, s % 2
+            return outs[q][512 * g : 512 * (g + 1), :].rearrange("(p t) c -> p t c", t=T)[:, 2 * e : 2 * e + 2, :]
 
-        def val_out(g, t):
+        def val_copy(s, t):
             if t == 0:
-                ovs[g] = ovp.tile([P, T, 512], F32, name="ov", tag="ov")
-            nc.scalar.copy(out=ovs[g][:, t, :], in_=banks["val", g, t][:])
+                ovs[s] = ovp.tile([P, 2, 512], F32, name="ov", tag="ov")
+            nc.scalar.copy(out=ovs[s][:, t, :], in_=banks["val", s, t][:])
 
-        def val_finish(g, t0):
-            ov = ovs[g][:, t0 : t0 + 2, :]
+        def val_finish(s):
+            ov = ovs[s][:]
             nc.gpsimd.tensor_tensor(
                 out=ov, in0=ov, in1=bias_bc[:, 512:1024].unsqueeze(1).to_broadcast([P, 2, 512]), op=ALU.add
             )
-            nc.sync.dma_start(out=out_rows(2, g, t0), in_=ov)
+            nc.sync.dma_start(out=out_rows(2, s), in_=ov)
 
-        pass_bias = bias_bc[:, 0:512].rearrange("p (q h j) -> p q h j", q=2, h=8)
+        def half(s, t, c0):
+            if s not in oqk:
+                oqk[s] = oqkp.tile([P, 2, 2, 512], F32, name="oqk", tag="oqk")
+            return oqk[s][:, :, t, :].rearrange("p q (h d) -> p q h d", d=64)[:, :, :, c0 : c0 + 32]
 
-        def half(g, t, c0):
-            return oqk[g][:, :, t, :].rearrange("p q (h d) -> p q h d", d=64)[:, :, :, c0 : c0 + 32]
+        def pass_out(s, t):
+            nc.vector.tensor_tensor(
+                out=half(s, t, 32),
+                in0=banks["pass", s, t][:].rearrange("p (q h j) -> p q h j", q=2, h=8),
+                in1=bias_bc[:, 0:512].rearrange("p (q h j) -> p q h j", q=2, h=8),
+                op=ALU.add,
+            )
 
-        def pass_out(g, t, on_vector):
-            if g not in oqk:
-                oqk[g] = oqkp.tile([P, 2, T, 512], F32, name="oqk", tag="oqk")
-            bv = banks["pass", g, t][:].rearrange("p (q h j) -> p q h j", q=2, h=8)
-            if on_vector:
-                nc.vector.tensor_tensor(out=half(g, t, 32), in0=bv, in1=pass_bias, op=ALU.add)
-            else:
-                nc.scalar.copy(out=half(g, t, 32), in_=bv)
+        def back(s):
+            for t in range(2):
+                bt = pss.tile([P, 512], F32, name="bt", tag="s")
+                for i in range(4):
+                    for part, moving in ((0, ident_f), (1, perm_f)):
+                        nc.tensor.matmul(
+                            bt[:, P * i : P * (i + 1)],
+                            lhsT=mw[s, i][:, part, P * t : P * (t + 1)], rhs=moving[:],
+                            is_transpose=True, start=(part == 0), stop=(part == 1),
+                        )
+                nc.scalar.copy(out=half(s, t, 0), in_=bt[:].rearrange("p (q h j) -> p q h j", q=2, h=8))
 
-        def pass_finish(g, t):
-            nc.gpsimd.tensor_tensor(out=half(g, t, 32), in0=half(g, t, 32), in1=pass_bias, op=ALU.add)
-
-        def back_tile(g, t):
-            bt = pss.tile([P, 512], F32, name="bt", tag="s")
-            for i in range(4):
-                for part, moving in ((0, ident_f), (1, perm_f)):
-                    nc.tensor.matmul(
-                        bt[:, P * i : P * (i + 1)],
-                        lhsT=mw[(g, i)][:, part, P * t : P * (t + 1)], rhs=moving[:],
-                        is_transpose=True, start=(part == 0), stop=(part == 1),
-                    )
-            nc.scalar.copy(out=half(g, t, 0), in_=bt[:].rearrange("p (q h j) -> p q h j", q=2, h=8))
-
-        def store_qk(g, t0):
+        def store_qk(s):
             for q in range(2):
-                nc.sync.dma_start(out=out_rows(q, g, t0), in_=oqk[g][:, q, t0 : t0 + 2, :])
+                nc.sync.dma_start(out=out_rows(q, s), in_=oqk[s][:, q])
 
-        def val_tile(g, t):
-            token_mm("val", g, t, False)
-            val_out(g, t)
+        def val_tile(s, t):
+            token_mm("val", s, t)
+            val_copy(s, t)
 
-        def round_end(g):
-            token_mm("pass", g, 3, True)
-            pass_out(g, 2, True)
-            turn_mm(g + 1, 0)
-            turn_mm(g + 1, 1)
-            pass_out(g, 3, True)
-            for t in range(T):
-                back_tile(g, t)
-                if t % 2 == 1:
-                    store_qk(g, t - 1)
-
+        x_transposes(0)
+        x_copy_out(0)
+        x_quantise(0)
+        pbv = bias_row_mm(bnat[:, 1024:1536])
+        nc.scalar.copy(out=bias_bc[:, 512:1024], in_=pbv[:])
+        nc.vector.tensor_copy(
+            out=wg[:, VAL : VAL + 512, :].rearrange("q (c i) t -> q c t i", i=4),
+            in_=wraw[2][:].rearrange("q t (c i) -> q c t i", i=4),
+        )
+        nc.vector.tensor_copy(
+            out=brow[:].rearrange("p (w g j) -> p w g j", w=2, g=16),
+            in_=bnat[:, 0:1024].rearrange("p (g w j) -> p w g j", g=16, w=2),
+        )
+        w_quantise(VAL)
+        pbp = bias_row_mm(brow[:, 512:1024])
+        pbt = psv.tile([P, 512], F32, name="pbt", tag="v")
+        for i in range(4):
+            nc.tensor.matmul(
+                pbt[:, 32 * i : 32 * (i + 1)], lhsT=brow[:, P * i : P * (i + 1)], rhs=ones_b[:, 0:32],
+                start=True, stop=True,
+            )
+        spread_scalar(0, 4)
+        nc.scalar.copy(out=bias_bc[:, 0:512], in_=pbp[:])
+        w_half(nc.vector.tensor_copy, 0, 0)
+        w_half(nc.vector.tensor_copy, 1, 0)
+        nc.vector.tensor_copy(
+            out=biasT[:], in_=pbt[:, 0:128].rearrange("p (i n) -> p i n", n=32)[:, :, 0]
+        )
         val_tile(0, 0)
-        val_tile(0, 1)
-        val_finish(0, 0)
-        val_tile(0, 2)
-        turn_mm(0, 0)
-        turn_mm(0, 1)
-        val_tile(0, 3)
-        val_finish(0, 2)
-        turn_mm(0, 2)
-        turn(0, 0)
-        turn_mm(0, 3)
-        turn(0, 1)
+        table_part(0)
+        token_mm("val", 0, 1)
         x_transposes(1)
         x_copy_out(1)
-        table_part(1)
-        token_mm("pass", 0, 1, True)
-        turn(0, 2)
-        token_mm("pass", 0, 2, True)
-        turn(0, 3)
+        val_copy(0, 1)
+        w_quantise(ROT)
+        w_half(nc.vector.tensor_copy, 0, 1)
+        turn_mm(0, 0)
+        turn_mm(0, 1)
         x_quantise(1)
-        token_mm("pass", 0, 0, False)
-        pass_out(0, 0, False)
-        pass_finish(0, 0)
-        pass_out(0, 1, True)
+        val_finish(0)
+        w_half(nc.scalar.copy, 1, 1)
         x_transposes(2)
         x_copy_out(2)
-        round_end(0)
-        table_part(2)
-        table_part(3)
+        spread_scalar(4, 4)
+        for i in range(4):
+            turn(0, i)
+        w_quantise(PAS)
+        turn_mm(1, 0)
+        turn_mm(1, 1)
 
-        for g in range(1, GROUPS):
-            turn_mm(g, 2)
-            turn(g, 0)
-            x_quantise(g + 1)
-            val_tile(g, 0)
-            turn_mm(g, 3)
-            turn(g, 1)
-            val_tile(g, 1)
-            val_finish(g, 0)
-            val_tile(g, 2)
-            token_mm("pass", g, 1, True)
-            turn(g, 2)
-            val_tile(g, 3)
-            val_finish(g, 2)
-            token_mm("pass", g, 2, True)
-            turn(g, 3)
-            x_transposes(g + 2)
-            x_copy_out(g + 2)
-            token_mm("pass", g, 0, False)
-            pass_out(g, 0, False)
-            pass_finish(g, 0)
-            pass_out(g, 1, True)
-            round_end(g)
+        val_tile(1, 0)
+        val_tile(1, 1)
+        val_finish(1)
+        back(0)
+        turn(1, 0)
+        x_quantise(2)
+        turn(1, 1)
+        token_mm("pass", 0, 0)
+        token_mm("pass", 0, 1)
+        pass_out(0, 0)
+        pass_out(0, 1)
+        store_qk(0)
+        table_part(1)
+        x_split(3)
+        turn(1, 2)
+        turn(1, 3)
+        token_mm("pass", 1, 0)
+        token_mm("pass", 1, 1)
+        x_transposes(3)
+        x_copy_out(3)
+        x_split(4)
+        pass_out(1, 0)
+        pass_out(1, 1)
+        turn_mm(2, 0)
+        turn_mm(2, 1)
+        spread_gpsimd(8, 8)
+
+        for s in range(2, STEPS):
+            val_tile(s, 0)
+            val_tile(s, 1)
+            val_finish(s)
+            token_mm("pass", s, 0)
+            token_mm("pass", s, 1)
+            turn(s, 0)
+            x_quantise(s + 1)
+            for i in range(1, 4):
+                turn(s, i)
+            back(s - 1)
+            store_qk(s - 1)
+            x_transposes(s + 2)
+            x_copy_out(s + 2)
+            x_split(s + 3)
+            pass_out(s, 0)
+            pass_out(s, 1)
+            turn_mm(s + 1, 0)
+            turn_mm(s + 1, 1)
+            if s in (2, 4):
+                table_part(s // 2 + 1)
+        back(STEPS - 1)
+        store_qk(STEPS - 1)

@@ -64,12 +64,13 @@ def tile_improvedattention_pa_t_kernel(
                 in_=W_qkv[:, 512 * n : 512 * (n + 1)].rearrange("(q t) c -> q t c", t=4),
             )
 
-        for hf in range(2):
+        def load_x0(hf):
             cols = slice(2 * E * hf, 2 * E * (hf + 1))
             nc.sync.dma_start(out=x_sb[0][:, cols], in_=x_rows(0)[:, cols])
-            if hf == 0:
-                load_w(2)
-                nc.sync.dma_start(out=bnat[0:1, :], in_=b_qkv.rearrange("(o c) -> o c", o=1))
+
+        load_x0(0)
+        load_w(2)
+        nc.sync.dma_start(out=bnat[0:1, :], in_=b_qkv.rearrange("(o c) -> o c", o=1))
         for tab_sb, tab in ((stab, sin_tab), (ctab, cos_tab)):
             nc.sync.dma_start(
                 out=tab_sb[:].rearrange("p (g t) j -> p g (t j)", g=4),
@@ -77,6 +78,7 @@ def tile_improvedattention_pa_t_kernel(
             )
         load_w(0)
         load_w(1)
+        load_x0(1)
         for g in range(1, GROUPS):
             nc.sync.dma_start(out=x_sb[g][:], in_=x_rows(g))
 
@@ -91,6 +93,20 @@ def tile_improvedattention_pa_t_kernel(
         pm4 = perm_f[:].rearrange("p (a w i) -> p a w i", a=4, w=2)
         nc.vector.tensor_copy(out=pm4[:, :, 0, :], in_=id4[:, :, 1, :])
         nc.vector.tensor_copy(out=pm4[:, :, 1, :], in_=id4[:, :, 0, :])
+
+        sel = const.tile([P, 2, T, P], BF16, name="sel")
+        idt = ident_b[:].rearrange("p (t j) -> p t j", t=T)
+        sel_c = sel[:, 0].rearrange("p t (r j) -> p t r j", r=4)
+        sel_s = sel[:, 1].rearrange("p t (r w i) -> p t r w i", r=4, w=2)
+        for out, src, sign in (
+            (sel_c, idt, 1.0),
+            (sel_s[:, :, :, 0, :], idt[:, :, 16:32], 1.0),
+            (sel_s[:, :, :, 1, :], idt[:, :, 0:16], -1.0),
+        ):
+            nc.gpsimd.tensor_scalar(
+                out=out, in0=src.unsqueeze(2).to_broadcast([P, T, 4, src.shape[2]]),
+                scalar1=sign, scalar2=0.0, op0=ALU.mult, op1=ALU.add,
+            )
 
         xc = {}
         xs = {}
@@ -137,12 +153,10 @@ def tile_improvedattention_pa_t_kernel(
         brow = const.tile([P, 1024], BF16, name="brow")
         bias_bc = const.tile([P, 1024], F32, name="bias_bc")
         biasT = const.tile([P, 4], F32, name="biasT")
-        csrep = const.tile([P, 2, 16, P], BF16, name="csrep")
+        tabT = const.tile([P, 2, 4, P], BF16, name="tabT")
         csT = []
         for gp in range(4):
             csT.append(const.tile([P, 2, 512], BF16, name="csT%d" % gp))
-        crep = csrep[:, 0].rearrange("p a (r j) -> p a r j", r=4)
-        srep = csrep[:, 1].rearrange("p a (r w i) -> p a r w i", r=4, w=2)
         wg = const.tile([P, 3 * E, 4], BF16, name="wg", align_bytes=64)
         wc = const.tile([P, 3 * E], U32, name="wc", align_bytes=64)
         ws = const.tile([P, 3 * E], U8, name="ws", align_bytes=64)
@@ -152,30 +166,25 @@ def tile_improvedattention_pa_t_kernel(
             nc.tensor.matmul(pb[:], lhsT=ones_b[:], rhs=rhs, start=True, stop=True)
             return pb
 
-        def spread(tab_part, n, width):
-            return tab_part.unsqueeze(2).to_broadcast([P, n, 4, width])
+        def tables_turn():
+            pt = pss.tile([P, 2, 4, P], BF16, name="pt", tag="s")
+            for n, tab_sb in enumerate((ctab, stab)):
+                for gp in range(4):
+                    rows = tab_sb[:, T * gp : T * (gp + 1), :].rearrange("p t j -> p (t j)")
+                    nc.tensor.transpose(pt[:, n, gp, :], rows, ident_b[:])
+            return pt
 
-        def spread_scalar(a0, n):
-            a = slice(a0, a0 + n)
-            nc.scalar.copy(out=crep[:, a], in_=spread(ctab[:, a, :], n, 32))
-            nc.scalar.copy(out=srep[:, a, :, 0, :], in_=spread(stab[:, a, 16:32], n, 16))
-            nc.scalar.mul(out=srep[:, a, :, 1, :], in_=spread(stab[:, a, 0:16], n, 16), mul=-1.0)
-
-        def spread_gpsimd(a0, n):
-            a = slice(a0, a0 + n)
-            for out, src, sign in (
-                (crep[:, a], spread(ctab[:, a, :], n, 32), 1.0),
-                (srep[:, a, :, 0, :], spread(stab[:, a, 16:32], n, 16), 1.0),
-                (srep[:, a, :, 1, :], spread(stab[:, a, 0:16], n, 16), -1.0),
-            ):
-                nc.gpsimd.tensor_scalar(out=out, in0=src, scalar1=sign, scalar2=0.0, op0=ALU.mult, op1=ALU.add)
-
-        def table_part(gp):
-            pt = pss.tile([P, 2, T, P], BF16, name="pt", tag="s")
-            for tab in range(2):
+        def table_mm(gp):
+            pc = pss.tile([P, 2, T, P], BF16, name="pc", tag="s")
+            for n in range(2):
                 for t in range(T):
-                    nc.tensor.transpose(pt[:, tab, t, :], csrep[:, tab, T * gp + t, :], ident_b[:])
-            nc.scalar.copy(out=csT[gp][:], in_=pt[:].rearrange("p b t c -> p b (t c)"))
+                    nc.tensor.matmul(
+                        pc[:, n, t, :], lhsT=sel[:, n, t, :], rhs=tabT[:, n, gp, :], start=True, stop=True
+                    )
+            return pc
+
+        def table_out(gp, pc):
+            nc.scalar.copy(out=csT[gp][:], in_=pc[:].rearrange("p b t c -> p b (t c)"))
 
         def w_quantise(c0):
             nc.vector.quantize_mx(
@@ -249,7 +258,9 @@ def tile_improvedattention_pa_t_kernel(
             nc.gpsimd.tensor_tensor(
                 out=ov, in0=ov, in1=bias_bc[:, 512:1024].unsqueeze(1).to_broadcast([P, 2, 512]), op=ALU.add
             )
-            nc.sync.dma_start(out=out_rows(2, s), in_=ov)
+
+        def store_val(s):
+            nc.sync.dma_start(out=out_rows(2, s), in_=ovs[s][:])
 
         def half(s, t, c0):
             if s not in oqk:
@@ -286,9 +297,6 @@ def tile_improvedattention_pa_t_kernel(
 
         x_transposes(0)
         x_copy_out(0)
-        x_quantise(0)
-        pbv = bias_row_mm(bnat[:, 1024:1536])
-        nc.scalar.copy(out=bias_bc[:, 512:1024], in_=pbv[:])
         nc.vector.tensor_copy(
             out=wg[:, VAL : VAL + 512, :].rearrange("q (c i) t -> q c t i", i=4),
             in_=wraw[2][:].rearrange("q t (c i) -> q c t i", i=4),
@@ -297,69 +305,77 @@ def tile_improvedattention_pa_t_kernel(
             out=brow[:].rearrange("p (w g j) -> p w g j", w=2, g=16),
             in_=bnat[:, 0:1024].rearrange("p (g w j) -> p w g j", g=16, w=2),
         )
+        pbv = bias_row_mm(bnat[:, 1024:1536])
+        x_quantise(0)
         w_quantise(VAL)
-        pbp = bias_row_mm(brow[:, 512:1024])
+        pt = tables_turn()
         pbt = psv.tile([P, 512], F32, name="pbt", tag="v")
         for i in range(4):
             nc.tensor.matmul(
                 pbt[:, 32 * i : 32 * (i + 1)], lhsT=brow[:, P * i : P * (i + 1)], rhs=ones_b[:, 0:32],
                 start=True, stop=True,
             )
-        spread_scalar(0, 4)
-        nc.scalar.copy(out=bias_bc[:, 0:512], in_=pbp[:])
+        pbp = bias_row_mm(brow[:, 512:1024])
         w_half(nc.vector.tensor_copy, 0, 0)
+        w_half(nc.vector.tensor_copy, 0, 1)
+        nc.scalar.copy(out=bias_bc[:, 0:512], in_=pbp[:])
+        nc.scalar.copy(out=tabT[:], in_=pt[:])
+        token_mm("val", 0, 0)
+        token_mm("val", 0, 1)
+        pc = table_mm(0)
+        val_copy(0, 0)
+        nc.scalar.copy(out=bias_bc[:, 512:1024], in_=pbv[:])
+        table_out(0, pc)
         w_half(nc.vector.tensor_copy, 1, 0)
         nc.vector.tensor_copy(
             out=biasT[:], in_=pbt[:, 0:128].rearrange("p (i n) -> p i n", n=32)[:, :, 0]
         )
-        val_tile(0, 0)
-        table_part(0)
-        token_mm("val", 0, 1)
         x_transposes(1)
         x_copy_out(1)
         val_copy(0, 1)
+        val_finish(0)
         w_quantise(ROT)
-        w_half(nc.vector.tensor_copy, 0, 1)
+        x_quantise(1)
         turn_mm(0, 0)
         turn_mm(0, 1)
-        x_quantise(1)
-        val_finish(0)
+        turn(0, 0)
         w_half(nc.scalar.copy, 1, 1)
         x_transposes(2)
-        x_copy_out(2)
-        spread_scalar(4, 4)
-        for i in range(4):
+        for i in range(1, 4):
             turn(0, i)
+        store_val(0)
         w_quantise(PAS)
         turn_mm(1, 0)
         turn_mm(1, 1)
+        x_copy_out(2)
 
-        val_tile(1, 0)
-        val_tile(1, 1)
-        val_finish(1)
+        x_split(3)
         back(0)
-        turn(1, 0)
-        x_quantise(2)
-        turn(1, 1)
         token_mm("pass", 0, 0)
         token_mm("pass", 0, 1)
+        turn(1, 0)
+        turn(1, 1)
+        x_quantise(2)
+        val_tile(1, 0)
+        val_tile(1, 1)
+        turn(1, 2)
+        turn(1, 3)
+        x_transposes(3)
+        pc = table_mm(1)
+        table_out(1, pc)
         pass_out(0, 0)
         pass_out(0, 1)
         store_qk(0)
-        table_part(1)
-        x_split(3)
-        turn(1, 2)
-        turn(1, 3)
+        val_finish(1)
         token_mm("pass", 1, 0)
         token_mm("pass", 1, 1)
-        x_transposes(3)
-        x_copy_out(3)
-        x_split(4)
-        pass_out(1, 0)
-        pass_out(1, 1)
         turn_mm(2, 0)
         turn_mm(2, 1)
-        spread_gpsimd(8, 8)
+        x_split(4)
+        x_copy_out(3)
+        pass_out(1, 0)
+        pass_out(1, 1)
+        store_val(1)
 
         for s in range(2, STEPS):
             val_tile(s, 0)
@@ -373,14 +389,17 @@ def tile_improvedattention_pa_t_kernel(
                 turn(s, i)
             back(s - 1)
             store_qk(s - 1)
+            store_val(s)
             x_transposes(s + 2)
             x_copy_out(s + 2)
+            if s in (2, 4):
+                gp = s // 2 + 1
+                pc = table_mm(gp)
+                table_out(gp, pc)
             x_split(s + 3)
             pass_out(s, 0)
             pass_out(s, 1)
             turn_mm(s + 1, 0)
             turn_mm(s + 1, 1)
-            if s in (2, 4):
-                table_part(s // 2 + 1)
         back(STEPS - 1)
         store_qk(STEPS - 1)

@@ -13,8 +13,8 @@ ALU = mybir.AluOpType
 P = 128
 TOKENS = 4096
 E = 512
-GROUPS = 8
-T = 4
+BATCH = 2048
+T = 16
 STEPS = 16
 N = 256
 FLOPS = 2 * TOKENS * E * 3 * E
@@ -31,7 +31,7 @@ def tile_improvedattention_pa_t_kernel(
 
     with ExitStack() as ctx:
         const = ctx.enter_context(tc.tile_pool(name="const", bufs=1))
-        xin = ctx.enter_context(tc.tile_pool(name="xin", bufs=GROUPS))
+        xin = ctx.enter_context(tc.tile_pool(name="xin", bufs=1))
         xpp = ctx.enter_context(tc.tile_pool(name="xpp", bufs=2))
         xgr = ctx.enter_context(tc.tile_pool(name="xgr", bufs=3))
         xq = ctx.enter_context(tc.tile_pool(name="xq", bufs=5))
@@ -48,15 +48,9 @@ def tile_improvedattention_pa_t_kernel(
         ctab = const.tile([P, 16, 32], BF16, name="ctab")
         stab = const.tile([P, 16, 32], BF16, name="stab")
 
-        x_sb = []
-        for g in range(GROUPS):
-            x_sb.append(xin.tile([P, T * E], BF16, name="x_sb%d" % g, tag="x_sb"))
         wraw = []
         for n in range(3):
             wraw.append(const.tile([P, 4, 512], BF16, name="wraw%d" % n))
-
-        def x_rows(g):
-            return xf[512 * g : 512 * (g + 1), :].rearrange("(p t) k -> p (t k)", t=T)
 
         def load_w(n):
             nc.sync.dma_start(
@@ -64,23 +58,28 @@ def tile_improvedattention_pa_t_kernel(
                 in_=W_qkv[:, 512 * n : 512 * (n + 1)].rearrange("(q t) c -> q t c", t=4),
             )
 
-        def load_x0(hf):
-            cols = slice(2 * E * hf, 2 * E * (hf + 1))
-            nc.sync.dma_start(out=x_sb[0][:, cols], in_=x_rows(0)[:, cols])
+        x_step = []
 
-        load_x0(0)
+        def load_x(steps):
+            s0 = len(x_step)
+            xt = xin.tile([P, steps * 2 * E], BF16, name="x%d" % s0, tag="x%d" % s0)
+            b, s1 = s0 // 8, s0 % 8
+            rows = xf[BATCH * b : BATCH * (b + 1), :].rearrange("(p t) k -> p (t k)", t=T)
+            nc.sync.dma_start(out=xt[:], in_=rows[:, 2 * E * s1 : 2 * E * (s1 + steps)])
+            for s in range(steps):
+                x_step.append(xt[:, 2 * E * s : 2 * E * (s + 1)])
+
+        load_x(1)
         load_w(2)
         nc.sync.dma_start(out=bnat[0:1, :], in_=b_qkv.rearrange("(o c) -> o c", o=1))
         for tab_sb, tab in ((stab, sin_tab), (ctab, cos_tab)):
             nc.sync.dma_start(
-                out=tab_sb[:].rearrange("p (g t) j -> p g (t j)", g=4),
-                in_=tab.rearrange("(g p t) j -> p g (t j)", g=4, p=P, t=T),
+                out=tab_sb[:].rearrange("p t j -> p (t j)"), in_=tab.rearrange("(p t) j -> p (t j)", t=T)
             )
         load_w(0)
         load_w(1)
-        load_x0(1)
-        for g in range(1, GROUPS):
-            nc.sync.dma_start(out=x_sb[g][:], in_=x_rows(g))
+        for steps in (1, 2, 4, 4, 4):
+            load_x(steps)
 
         ident_f = const.tile([P, P], F32, name="ident_f")
         make_identity(nc, ident_f[:])
@@ -94,8 +93,8 @@ def tile_improvedattention_pa_t_kernel(
         nc.vector.tensor_copy(out=pm4[:, :, 0, :], in_=id4[:, :, 1, :])
         nc.vector.tensor_copy(out=pm4[:, :, 1, :], in_=id4[:, :, 0, :])
 
-        sel = const.tile([P, 2, T, P], BF16, name="sel")
-        idt = ident_b[:].rearrange("p (t j) -> p t j", t=T)
+        sel = const.tile([P, 2, 4, P], BF16, name="sel")
+        idt = ident_b[:].rearrange("p (t j) -> p t j", t=4)
         sel_c = sel[:, 0].rearrange("p t (r j) -> p t r j", r=4)
         sel_s = sel[:, 1].rearrange("p t (r w i) -> p t r w i", r=4, w=2)
         for out, src, sign in (
@@ -104,7 +103,7 @@ def tile_improvedattention_pa_t_kernel(
             (sel_s[:, :, :, 1, :], idt[:, :, 0:16], -1.0),
         ):
             nc.gpsimd.tensor_scalar(
-                out=out, in0=src.unsqueeze(2).to_broadcast([P, T, 4, src.shape[2]]),
+                out=out, in0=src.unsqueeze(2).to_broadcast([P, 4, 4, src.shape[2]]),
                 scalar1=sign, scalar2=0.0, op0=ALU.mult, op1=ALU.add,
             )
 
@@ -115,7 +114,7 @@ def tile_improvedattention_pa_t_kernel(
         xgrouped = {}
 
         def x_words(s):
-            return x_sb[s // 2][:].bitcast(F32)[:, 512 * (s % 2) : 512 * (s % 2 + 1)]
+            return x_step[s].bitcast(F32)
 
         def x_split(s):
             if s < STEPS:
@@ -170,14 +169,14 @@ def tile_improvedattention_pa_t_kernel(
             pt = pss.tile([P, 2, 4, P], BF16, name="pt", tag="s")
             for n, tab_sb in enumerate((ctab, stab)):
                 for gp in range(4):
-                    rows = tab_sb[:, T * gp : T * (gp + 1), :].rearrange("p t j -> p (t j)")
+                    rows = tab_sb[:, 4 * gp : 4 * (gp + 1), :].rearrange("p t j -> p (t j)")
                     nc.tensor.transpose(pt[:, n, gp, :], rows, ident_b[:])
             return pt
 
         def table_mm(gp):
-            pc = pss.tile([P, 2, T, P], BF16, name="pc", tag="s")
+            pc = pss.tile([P, 2, 4, P], BF16, name="pc", tag="s")
             for n in range(2):
-                for t in range(T):
+                for t in range(4):
                     nc.tensor.matmul(
                         pc[:, n, t, :], lhsT=sel[:, n, t, :], rhs=tabT[:, n, gp, :], start=True, stop=True
                     )
@@ -245,8 +244,8 @@ def tile_improvedattention_pa_t_kernel(
             banks[kind, s, t] = bank
 
         def out_rows(q, s):
-            g, e = s // 2, s % 2
-            return outs[q][512 * g : 512 * (g + 1), :].rearrange("(p t) c -> p t c", t=T)[:, 2 * e : 2 * e + 2, :]
+            b, t0 = s // 8, 2 * (s % 8)
+            return outs[q][BATCH * b : BATCH * (b + 1), :].rearrange("(p t) c -> p t c", t=T)[:, t0 : t0 + 2, :]
 
         def val_copy(s, t):
             if t == 0:
@@ -380,6 +379,7 @@ def tile_improvedattention_pa_t_kernel(
         for s in range(2, STEPS):
             val_tile(s, 0)
             val_tile(s, 1)
+            x_split(s + 3)
             val_finish(s)
             token_mm("pass", s, 0)
             token_mm("pass", s, 1)
@@ -396,7 +396,6 @@ def tile_improvedattention_pa_t_kernel(
                 gp = s // 2 + 1
                 pc = table_mm(gp)
                 table_out(gp, pc)
-            x_split(s + 3)
             pass_out(s, 0)
             pass_out(s, 1)
             turn_mm(s + 1, 0)

@@ -294,8 +294,18 @@ def tile_improvedattention_pa_t_kernel(
             token_mm("val", s, t)
             val_copy(s, t)
 
+        warm = const.tile([P, 512], BF16, name="warm")
+        nc.vector.memset(warm[:], 1.0)
+
+        def warm_up(n):
+            pw = psv.tile([P, 512], F32, name="pw", tag="v")
+            for i in range(n):
+                nc.tensor.matmul(pw[:], lhsT=ones_b[:], rhs=warm[:], start=True, stop=True)
+
+        warm_up(3)
         x_transposes(0)
         x_copy_out(0)
+        warm_up(3)
         nc.vector.tensor_copy(
             out=wg[:, VAL : VAL + 512, :].rearrange("q (c i) t -> q c t i", i=4),
             in_=wraw[2][:].rearrange("q t (c i) -> q c t i", i=4),
@@ -305,6 +315,7 @@ def tile_improvedattention_pa_t_kernel(
             in_=bnat[:, 0:1024].rearrange("p (g w j) -> p w g j", g=16, w=2),
         )
         pbv = bias_row_mm(bnat[:, 1024:1536])
+        warm_up(1)
         x_quantise(0)
         w_quantise(VAL)
         pt = tables_turn()

from contextlib import ExitStack

import concourse.mybir as mybir
from concourse.masks import make_identity

F32 = mybir.dt.float32
BF16 = mybir.dt.bfloat16
U32 = mybir.dt.uint32
U8 = mybir.dt.uint8
FP8X4 = mybir.dt.float8_e4m3fn_x4
ALU = mybir.AluOpType

P = 128
TOKENS = 4096
E = 512
BATCH = 2048
T = 16
STEPS = 16
N = 256
FLOPS = 2 * TOKENS * E * 3 * E

ROT, PAS, VAL = 0, 512, 1024


def tile_improvedattention_pa_t_kernel(
    tc, x, W_qkv, b_qkv, sin_tab, cos_tab, out_0, out_1, out_2
):
    nc = tc.nc
    xf = x.flatten_outer_dims()
    outs = [o.rearrange("b s h d -> (b s) (h d)") for o in (out_0, out_1, out_2)]

    with ExitStack() as ctx:
        const = ctx.enter_context(tc.tile_pool(name="const", bufs=1))
        xin = ctx.enter_context(tc.tile_pool(name="xin", bufs=1))
        xpp = ctx.enter_context(tc.tile_pool(name="xpp", bufs=2))
        xgr = ctx.enter_context(tc.tile_pool(name="xgr", bufs=3))
        xq = ctx.enter_context(tc.tile_pool(name="xq", bufs=5))
        mwp = ctx.enter_context(tc.tile_pool(name="mwp", bufs=3))
        oqkp = ctx.enter_context(tc.tile_pool(name="oqkp", bufs=6))
        ovp = ctx.enter_context(tc.tile_pool(name="ovp", bufs=6))
        psv = ctx.enter_context(tc.psum_pool(name="psv", bufs=4))
        pss = ctx.enter_context(tc.psum_pool(name="pss", bufs=4))
        ctx.enter_context(nc.allow_non_contiguous_dma(reason="short rows of tables and column chunks"))
        ctx.enter_context(tc.manual_schedule())

        bnat = const.tile([P, 3 * E], BF16, name="bnat")
        nc.vector.memset(bnat[:].bitcast(U32), 0)
        ctab = const.tile([P, 16, 32], BF16, name="ctab")
        stab = const.tile([P, 16, 32], BF16, name="stab")

        wraw = []
        for n in range(3):
            wraw.append(const.tile([P, 4, 512], BF16, name="wraw%d" % n))

        def load_w(n):
            nc.sync.dma_start(
                out=wraw[n][:],
                in_=W_qkv[:, 512 * n : 512 * (n + 1)].rearrange("(q t) c -> q t c", t=4),
            )

        x_step = []

        def load_x(steps):
            s0 = len(x_step)
            xt = xin.tile([P, steps * 2 * E], BF16, name="x%d" % s0, tag="x%d" % s0)
            b, s1 = s0 // 8, s0 % 8
            rows = xf[BATCH * b : BATCH * (b + 1), :].rearrange("(p t) k -> p (t k)", t=T)
            nc.sync.dma_start(out=xt[:], in_=rows[:, 2 * E * s1 : 2 * E * (s1 + steps)])
            for s in range(steps):
                x_step.append(xt[:, 2 * E * s : 2 * E * (s + 1)])

        load_x(1)
        load_w(2)
        nc.sync.dma_start(out=bnat[0:1, :], in_=b_qkv.rearrange("(o c) -> o c", o=1))
        for tab_sb, tab in ((stab, sin_tab), (ctab, cos_tab)):
            nc.sync.dma_start(
                out=tab_sb[:].rearrange("p t j -> p (t j)"), in_=tab.rearrange("(p t) j -> p (t j)", t=T)
            )
        load_w(0)
        load_w(1)
        for steps in (1, 2, 4, 4, 4):
            load_x(steps)

        ident_f = const.tile([P, P], F32, name="ident_f")
        make_identity(nc, ident_f[:])
        ident_b = const.tile([P, P], BF16, name="ident_b")
        make_identity(nc, ident_b[:])
        ones_b = const.tile([P, P], BF16, name="ones_b")
        nc.vector.memset(ones_b[:], 1.0)
        perm_f = const.tile([P, P], F32, name="perm_f")
        id4 = ident_f[:].rearrange("p (a w i) -> p a w i", a=4, w=2)
        pm4 = perm_f[:].rearrange("p (a w i) -> p a w i", a=4, w=2)
        nc.vector.tensor_copy(out=pm4[:, :, 0, :], in_=id4[:, :, 1, :])
        nc.vector.tensor_copy(out=pm4[:, :, 1, :], in_=id4[:, :, 0, :])

        sel = const.tile([P, 2, 4, P], BF16, name="sel")
        idt = ident_b[:].rearrange("p (t j) -> p t j", t=4)
        sel_c = sel[:, 0].rearrange("p t (r j) -> p t r j", r=4)
        sel_s = sel[:, 1].rearrange("p t (r w i) -> p t r w i", r=4, w=2)
        for out, src, sign in (
            (sel_c, idt, 1.0),
            (sel_s[:, :, :, 0, :], idt[:, :, 16:32], 1.0),
            (sel_s[:, :, :, 1, :], idt[:, :, 0:16], -1.0),
        ):
            nc.gpsimd.tensor_scalar(
                out=out, in0=src.unsqueeze(2).to_broadcast([P, 4, 4, src.shape[2]]),
                scalar1=sign, scalar2=0.0, op0=ALU.mult, op1=ALU.add,
            )

        xc = {}
        xs = {}
        xperm = {}
        xbanks = {}
        xgrouped = {}

        def x_words(s):
            return x_step[s].bitcast(F32)

        def x_split(s):
            if s < STEPS:
                xperm[s] = xpp.tile([P, 2, 2, P], F32, name="xperm", tag="xperm")
                nc.scalar.copy(
                    out=xperm[s][:], in_=x_words(s).rearrange("p (t w u) -> p t u w", t=2, u=2)
                )

        def x_transposes(s):
            if s < STEPS:
                xt = pss.tile([P, 4, P], F32, name="xt", tag="s")
                for tt in range(2):
                    for u in range(2):
                        if s in xperm:
                            src = xperm[s][:, tt, u, :]
                        else:
                            src = x_words(s)[:, 256 * tt + u : 256 * (tt + 1) : 2]
                        nc.tensor.transpose(xt[:, 2 * tt + u, :], src, ident_f[:])
                xbanks[s] = xt

        def x_copy_out(s):
            if s < STEPS:
                xgrouped[s] = xgr.tile([P, 4 * N], BF16, name="grouped", tag="grouped", align_bytes=64)
                nc.scalar.copy(
                    out=xgrouped[s][:].bitcast(F32).rearrange("q (tt p u) -> q tt p u", tt=2, p=P, u=2),
                    in_=xbanks[s][:].rearrange("q (tt u) p -> q tt p u", tt=2, u=2),
                )

        def x_quantise(s):
            if s < STEPS:
                xc[s] = xq.tile([P, N], U32, name="xcodes", tag="xcodes", align_bytes=64)
                xs[s] = xq.tile([P, N], U8, name="xscales", tag="xscales", align_bytes=64)
                nc.vector.quantize_mx(out=xc[s][:].bitcast(FP8X4), scales=xs[s][:], in_=xgrouped[s][:])

        brow = const.tile([P, 1024], BF16, name="brow")
        bias_bc = const.tile([P, 1024], F32, name="bias_bc")
        biasT = const.tile([P, 4], F32, name="biasT")
        tabT = const.tile([P, 2, 4, P], BF16, name="tabT")
        csT = []
        for gp in range(4):
            csT.append(const.tile([P, 2, 512], BF16, name="csT%d" % gp))
        wg = const.tile([P, 3 * E, 4], BF16, name="wg", align_bytes=64)
        wc = const.tile([P, 3 * E], U32, name="wc", align_bytes=64)
        ws = const.tile([P, 3 * E], U8, name="ws", align_bytes=64)

        def bias_row_mm(rhs):
            pb = psv.tile([P, 512], F32, name="pb", tag="v")
            nc.tensor.matmul(pb[:], lhsT=ones_b[:], rhs=rhs, start=True, stop=True)
            return pb

        def tables_turn():
            pt = pss.tile([P, 2, 4, P], BF16, name="pt", tag="s")
            for n, tab_sb in enumerate((ctab, stab)):
                for gp in range(4):
                    rows = tab_sb[:, 4 * gp : 4 * (gp + 1), :].rearrange("p t j -> p (t j)")
                    nc.tensor.transpose(pt[:, n, gp, :], rows, ident_b[:])
            return pt

        def table_mm(gp):
            pc = pss.tile([P, 2, 4, P], BF16, name="pc", tag="s")
            for n in range(2):
                for t in range(4):
                    nc.tensor.matmul(
                        pc[:, n, t, :], lhsT=sel[:, n, t, :], rhs=tabT[:, n, gp, :], start=True, stop=True
                    )
            return pc

        def table_out(gp, pc):
            nc.scalar.copy(out=csT[gp][:], in_=pc[:].rearrange("p b t c -> p b (t c)"))

        def w_quantise(c0):
            nc.vector.quantize_mx(
                out=wc[:, c0 : c0 + 512].bitcast(FP8X4),
                scales=ws[:, c0 : c0 + 512],
                in_=wg[:, c0 : c0 + 512, :].rearrange("q c t -> q (c t)"),
            )

        def w_half(copy, n, w):
            c0 = (ROT, PAS)[w] + 256 * n
            copy(
                out=wg[:, c0 : c0 + 256, :].rearrange("q (g j) t -> q g j t", g=8),
                in_=wraw[n][:].rearrange("q t (g w j) -> q w g j t", g=8, w=2)[:, w],
            )

        oqk = {}
        ovs = {}
        mw = {}
        banks = {}

        def mx(out, lhsT, lhsT_scale, rhs, rhs_scale):
            nc.tensor.matmul_mx(
                out=out, lhsT=lhsT.bitcast(FP8X4), lhsT_scale=lhsT_scale,
                rhs=rhs.bitcast(FP8X4), rhs_scale=rhs_scale, start=True, stop=True,
            )

        def turn_mm(s, j):
            if s < STEPS:
                bank = psv.tile([P, 2, N], F32, name="rbank", tag="v")
                for e in range(2):
                    c0 = ROT + P * (2 * j + e)
                    cols = slice(c0, c0 + P)
                    mx(bank[:, e, :], wc[:, cols], ws[:, cols], xc[s][:], xs[s][:])
                banks["turn", s, j] = bank

        def turn(s, i):
            m = mwp.tile([P, 2, N], F32, name="mw%d" % i, tag="mw%d" % i)
            c0 = N * (s % 2)
            nc.vector.scalar_tensor_tensor(
                out=m[:],
                in0=banks["turn", s, i // 2][:, i % 2, :].unsqueeze(1).to_broadcast([P, 2, N]),
                scalar=biasT[:, i : i + 1],
                in1=csT[s // 2 % 4][:, :, c0 : c0 + N],
                op0=ALU.add,
                op1=ALU.mult,
            )
            mw[s, i] = m

        def token_mm(kind, s, t):
            if kind == "val":
                bank = pss.tile([P, 512], F32, name="vbank", tag="s")
                c0 = VAL
            else:
                bank = psv.tile([P, 512], F32, name="pbank", tag="v")
                c0 = PAS
            cols = slice(P * t, P * (t + 1))
            mx(bank[:], xc[s][:, cols], xs[s][:, cols], wc[:, c0 : c0 + 512], ws[:, c0 : c0 + 512])
            banks[kind, s, t] = bank

        def out_rows(q, s):
            b, t0 = s // 8, 2 * (s % 8)
            return outs[q][BATCH * b : BATCH * (b + 1), :].rearrange("(p t) c -> p t c", t=T)[:, t0 : t0 + 2, :]

        def val_copy(s, t):
            if t == 0:
                ovs[s] = ovp.tile([P, 2, 512], F32, name="ov", tag="ov")
            nc.scalar.copy(out=ovs[s][:, t, :], in_=banks["val", s, t][:])

        def val_finish(s):
            ov = ovs[s][:]
            nc.gpsimd.tensor_tensor(
                out=ov, in0=ov, in1=bias_bc[:, 512:1024].unsqueeze(1).to_broadcast([P, 2, 512]), op=ALU.add
            )

        def store_val(s):
            nc.sync.dma_start(out=out_rows(2, s), in_=ovs[s][:])

        def half(s, t, c0):
            if s not in oqk:
                oqk[s] = oqkp.tile([P, 2, 2, 512], F32, name="oqk", tag="oqk")
            return oqk[s][:, :, t, :].rearrange("p q (h d) -> p q h d", d=64)[:, :, :, c0 : c0 + 32]

        def pass_out(s, t):
            nc.vector.tensor_tensor(
                out=half(s, t, 32),
                in0=banks["pass", s, t][:].rearrange("p (q h j) -> p q h j", q=2, h=8),
                in1=bias_bc[:, 0:512].rearrange("p (q h j) -> p q h j", q=2, h=8),
                op=ALU.add,
            )

        def back(s):
            for t in range(2):
                bt = pss.tile([P, 512], F32, name="bt", tag="s")
                for i in range(4):
                    for part, moving in ((0, ident_f), (1, perm_f)):
                        nc.tensor.matmul(
                            bt[:, P * i : P * (i + 1)],
                            lhsT=mw[s, i][:, part, P * t : P * (t + 1)], rhs=moving[:],
                            is_transpose=True, start=(part == 0), stop=(part == 1),
                        )
                nc.scalar.copy(out=half(s, t, 0), in_=bt[:].rearrange("p (q h j) -> p q h j", q=2, h=8))

        def store_qk(s):
            for q in range(2):
                nc.sync.dma_start(out=out_rows(q, s), in_=oqk[s][:, q])

        def val_tile(s, t):
            token_mm("val", s, t)
            val_copy(s, t)

        warm = const.tile([P, 512], BF16, name="warm")
        nc.vector.memset(warm[:], 1.0)

        def warm_up(n):
            pw = psv.tile([P, 512], F32, name="pw", tag="v")
            for i in range(n):
                nc.tensor.matmul(pw[:], lhsT=ones_b[:], rhs=warm[:], start=True, stop=True)

        warm_up(3)
        x_transposes(0)
        x_copy_out(0)
        warm_up(3)
        nc.vector.tensor_copy(
            out=wg[:, VAL : VAL + 512, :].rearrange("q (c i) t -> q c t i", i=4),
            in_=wraw[2][:].rearrange("q t (c i) -> q c t i", i=4),
        )
        nc.vector.tensor_copy(
            out=brow[:].rearrange("p (w g j) -> p w g j", w=2, g=16),
            in_=bnat[:, 0:1024].rearrange("p (g w j) -> p w g j", g=16, w=2),
        )
        pbv = bias_row_mm(bnat[:, 1024:1536])
        warm_up(1)
        x_quantise(0)
        w_quantise(VAL)
        pt = tables_turn()
        pbt = psv.tile([P, 512], F32, name="pbt", tag="v")
        for i in range(4):
            nc.tensor.matmul(
                pbt[:, 32 * i : 32 * (i + 1)], lhsT=brow[:, P * i : P * (i + 1)], rhs=ones_b[:, 0:32],
                start=True, stop=True,
            )
        pbp = bias_row_mm(brow[:, 512:1024])
        w_half(nc.vector.tensor_copy, 0, 0)
        w_half(nc.vector.tensor_copy, 0, 1)
        nc.scalar.copy(out=bias_bc[:, 0:512], in_=pbp[:])
        nc.scalar.copy(out=tabT[:], in_=pt[:])
        token_mm("val", 0, 0)
        token_mm("val", 0, 1)
        pc = table_mm(0)
        val_copy(0, 0)
        nc.scalar.copy(out=bias_bc[:, 512:1024], in_=pbv[:])
        table_out(0, pc)
        w_half(nc.vector.tensor_copy, 1, 0)
        nc.vector.tensor_copy(
            out=biasT[:], in_=pbt[:, 0:128].rearrange("p (i n) -> p i n", n=32)[:, :, 0]
        )
        x_transposes(1)
        x_copy_out(1)
        val_copy(0, 1)
        val_finish(0)
        w_quantise(ROT)
        x_quantise(1)
        turn_mm(0, 0)
        turn_mm(0, 1)
        turn(0, 0)
        w_half(nc.scalar.copy, 1, 1)
        x_transposes(2)
        for i in range(1, 4):
            turn(0, i)
        store_val(0)
        w_quantise(PAS)
        turn_mm(1, 0)
        turn_mm(1, 1)
        x_copy_out(2)

        x_split(3)
        back(0)
        token_mm("pass", 0, 0)
        token_mm("pass", 0, 1)
        turn(1, 0)
        turn(1, 1)
        x_quantise(2)
        val_tile(1, 0)
        val_tile(1, 1)
        turn(1, 2)
        turn(1, 3)
        x_transposes(3)
        pc = table_mm(1)
        table_out(1, pc)
        pass_out(0, 0)
        pass_out(0, 1)
        store_qk(0)
        val_finish(1)
        token_mm("pass", 1, 0)
        token_mm("pass", 1, 1)
        turn_mm(2, 0)
        turn_mm(2, 1)
        x_split(4)
        x_copy_out(3)
        pass_out(1, 0)
        pass_out(1, 1)
        store_val(1)

        for s in range(2, STEPS):
            val_tile(s, 0)
            val_tile(s, 1)
            x_split(s + 3)
            val_finish(s)
            token_mm("pass", s, 0)
            token_mm("pass", s, 1)
            turn(s, 0)
            x_quantise(s + 1)
            for i in range(1, 4):
                turn(s, i)
            back(s - 1)
            store_qk(s - 1)
            store_val(s)
            x_transposes(s + 2)
            x_copy_out(s + 2)
            if s in (2, 4):
                gp = s // 2 + 1
                pc = table_mm(gp)
                table_out(gp, pc)
            pass_out(s, 0)
            pass_out(s, 1)
            turn_mm(s + 1, 0)
            turn_mm(s + 1, 1)
        back(STEPS - 1)
        store_qk(STEPS - 1)
